import numpy as np
import ml_dtypes


def mxq(x, axis, fmt="e4m3"):
    dtype, down = {"e4m3": (ml_dtypes.float8_e4m3fn, 7), "e5m2": (ml_dtypes.float8_e5m2, 14)}[fmt]
    v = np.moveaxis(np.asarray(x, np.float32).astype(ml_dtypes.bfloat16).astype(np.float64), axis, -1)
    blocks = v.reshape(v.shape[:-1] + (-1, 32))
    amax = np.abs(blocks).max(-1, keepdims=True)
    byte = np.maximum(np.where(amax > 0, np.frexp(amax)[1] - 1 + 127, 0) - down, 1)
    scale = np.exp2(byte - 127.0)
    codes = (blocks / scale).astype(np.float32).astype(dtype).astype(np.float64)
    return np.moveaxis((codes * scale).reshape(v.shape), -1, axis)


WIDE = False


def mx_kscale(k):
    if not WIDE:
        return np.ones(k)
    levels = np.array([30, -30])
    if k % 512:
        return np.exp2(np.random.permutation(np.resize(levels, k // 32))).repeat(32)
    a = np.empty((k // 512, 16))
    for p in range(k // 512):
        a[p, :8] = np.random.permutation(np.resize(levels, 8))
        for g in range(8):
            far = levels[np.abs(levels - a[p, g]) >= 10]
            a[p, g + 8] = far[np.random.randint(len(far))]
    return np.exp2(a.ravel()).repeat(32)


BF16 = ml_dtypes.bfloat16


def bf(x):
    return np.asarray(x, np.float32).astype(BF16)


def f64(x):
    return np.asarray(x).astype(np.float64)


B, S, I, Q = 512, 8, 1024, 1024
LN_EPS = 1e-5


def setup_inputs():
    s = mx_kscale(I)
    return {"language_features": bf(np.random.standard_normal((B, I)) * s),
            "W": bf(np.random.standard_normal((S, I, Q)) / np.sqrt(I) / s[None, :, None]),
            "b": bf(np.random.standard_normal((S, Q)) * 0.2),
            "amplitude_weights": bf(np.random.standard_normal((S, Q))),
            "phase_weights": bf(np.random.standard_normal((S, Q))),
            "ln_gamma": bf(1.0 + 0.1 * np.random.standard_normal(Q)),
            "ln_beta": bf(0.1 * np.random.standard_normal(Q))}


def reference(language_features, W, b, amplitude_weights, phase_weights, ln_gamma, ln_beta):
    xq = mxq(f64(language_features), 1, "e5m2")
    wq = mxq(f64(W), 1, "e5m2")
    states = (xq @ wq).transpose(1, 0, 2) + f64(b)[None, :, :]
    a = f64(amplitude_weights)
    e = np.exp(a - a.max(axis=0, keepdims=True))
    amplitudes = e / e.sum(axis=0, keepdims=True)
    mix = amplitudes * np.cos(f64(phase_weights))
    sup = states * mix[None, :, :]
    mean = sup.mean(axis=-1, keepdims=True)
    var = sup.var(axis=-1, keepdims=True)
    return (sup - mean) * (1.0 / np.sqrt(var + LN_EPS)) * f64(ln_gamma) + f64(ln_beta)

@@ -1,0 +1,441 @@
+import math
+from contextlib import ExitStack
+
+import concourse.mybir as mybir
+from concourse.masks import make_identity
+
+B, S, I, Q = 512, 8, 1024, 1024
+LN_EPS = 1e-5
+FLOPS = 2 * B * S * I * Q
+
+F32 = mybir.dt.float32
+BF16 = mybir.dt.bfloat16
+I32 = mybir.dt.int32
+U32 = mybir.dt.uint32
+U8 = mybir.dt.uint8
+FP8X4 = mybir.dt.float8_e5m2_x4
+ALU = mybir.AluOpType
+ACT = mybir.ActivationFunctionType
+AXIS = mybir.AxisListType
+
+P = 128
+PACK = 4
+K_PASS = P * PACK
+PASSES = I // K_PASS
+BANK = 512
+HALVES = Q // BANK
+CHUNKS = Q // P
+CHUNKS_PER_HALF = BANK // P
+ROW_TILES = B // P
+FOLDED = ROW_TILES - 1
+SPLIT = 3
+STEPS = ROW_TILES
+PIECES = S * PASSES * HALVES
+LOAD_AHEAD = 8
+COPY_AHEAD = 4
+QUANT_AHEAD = 3
+
+TWO_PI_HI = 6.28125
+TWO_PI_LO = 2.0 * math.pi - TWO_PI_HI
+SIN_FLOOR = -3.1415925
+
+
+def vector_columns(step):
+    if step < STEPS:
+        return 368
+    if step < 2 * STEPS:
+        return 176
+    return 0 if step % STEPS == 0 else 320
+
+
+def tile_quantumsuperposition_kernel(
+    tc, language_features, W, b, amplitude_weights, phase_weights, ln_gamma, ln_beta, out
+):
+    nc = tc.nc
+
+    with ExitStack() as ctx:
+        keep = ctx.enter_context(tc.tile_pool(name="keep", bufs=1))
+        stream = ctx.enter_context(tc.tile_pool(name="stream", bufs=2))
+        psum = ctx.enter_context(tc.psum_pool(name="psum", bufs=1))
+
+        def bank(index, shape, dtype):
+            return psum.tile(shape, dtype, name="bank%d" % index, tag="bank%d" % index)
+
+        ident_f32 = keep.tile([P, P], F32)
+        ident_bf16 = keep.tile([P, P], BF16)
+        make_identity(nc, ident_bf16[:])
+        make_identity(nc, ident_f32[:])
+
+        rows_ap = keep.tile([P, P], BF16)
+        rows_bg = keep.tile([P, P], BF16)
+        sc = S * CHUNKS
+        nc.vector.memset(rows_bg[:], 0.0)
+        nc.scalar.dma_start(out=rows_ap[0:sc, :], in_=amplitude_weights.rearrange("s (c p) -> (s c) p", p=P))
+        nc.scalar.dma_start(out=rows_ap[sc:P, :], in_=phase_weights.rearrange("s (c p) -> (s c) p", p=P))
+        nc.scalar.dma_start(out=rows_bg[0:sc, :], in_=b.rearrange("s (c p) -> (s c) p", p=P))
+        nc.scalar.dma_start(out=rows_bg[sc : sc + CHUNKS, :], in_=ln_gamma.rearrange("(c p) -> c p", p=P))
+
+        x_rows = keep.tile([P, ROW_TILES, I], BF16)
+        x_hbm = language_features.rearrange("(t p) k -> p t k", p=P)
+        for pair in range(ROW_TILES // 2):
+            nc.sync.dma_start(out=x_rows[:, 2 * pair : 2 * pair + 2, :], in_=x_hbm[:, 2 * pair : 2 * pair + 2, :])
+
+        one = keep.tile([P, 1], F32)
+        eps = keep.tile([P, 1], F32)
+        nc.vector.memset(one[:], 1.0)
+        nc.vector.tensor_scalar(out=eps[:], in0=one[:], scalar1=LN_EPS, scalar2=None, op0=ALU.mult)
+
+        split_cols = keep.tile([P, P], BF16)
+        nc.gpsimd.memset(split_cols[:], 0.0)
+        fold_rhs = keep.tile([P, FOLDED, Q], BF16)
+        nc.gpsimd.memset(fold_rhs[:], 0.0)
+
+        cols = bank(6, [P, 2 * P], BF16)
+        nc.tensor.transpose(cols[:, 0:P], rows_ap[:], ident_bf16[:])
+        nc.tensor.transpose(cols[:, P : 2 * P], rows_bg[:], ident_bf16[:])
+        small = keep.tile([P, 2 * P], F32)
+        nc.vector.tensor_copy(out=small[:], in_=cols[:])
+        amp_t = small[:, 0:sc]
+        phase_t = small[:, sc:P]
+        bias_t = small[:, P : P + sc]
+        gamma_t = small[:, P + sc : P + sc + CHUNKS]
+
+        top = keep.tile([P, 1, CHUNKS], F32)
+        nc.vector.tensor_reduce(
+            out=top[:, 0, :], in_=amp_t.rearrange("p (s c) -> p c s", c=CHUNKS), axis=AXIS.X, op=ALU.max
+        )
+        shifted = keep.tile([P, S, CHUNKS], F32)
+        nc.vector.tensor_tensor(
+            out=shifted[:],
+            in0=amp_t.rearrange("p (s c) -> p s c", c=CHUNKS),
+            in1=top[:].to_broadcast([P, S, CHUNKS]),
+            op=ALU.subtract,
+        )
+        expd = keep.tile([P, S, CHUNKS], F32)
+        nc.scalar.activation(out=expd[:], in_=shifted[:], func=ACT.Exp)
+        total = keep.tile([P, CHUNKS], F32)
+        nc.vector.tensor_reduce(out=total[:], in_=expd[:].rearrange("p s c -> p c s"), axis=AXIS.X, op=ALU.add)
+        inv_total = keep.tile([P, 1, CHUNKS], F32)
+        nc.vector.reciprocal(out=inv_total[:, 0, :], in_=total[:])
+        amplitudes = keep.tile([P, S, CHUNKS], F32)
+        nc.vector.tensor_tensor(
+            out=amplitudes[:], in0=expd[:], in1=inv_total[:].to_broadcast([P, S, CHUNKS]), op=ALU.mult
+        )
+
+        phase_abs = keep.tile([P, sc], F32)
+        nc.scalar.activation(out=phase_abs[:], in_=phase_t, func=ACT.Abs)
+        turns_f = keep.tile([P, sc], F32)
+        nc.vector.tensor_scalar(
+            out=turns_f[:], in0=phase_abs[:], scalar1=1.0 / (2.0 * math.pi), scalar2=0.25, op0=ALU.mult, op1=ALU.add
+        )
+        turns = keep.tile([P, sc], I32)
+        nc.vector.tensor_copy(out=turns[:], in_=turns_f[:])
+        rest_hi = keep.tile([P, sc], F32)
+        nc.vector.scalar_tensor_tensor(
+            out=rest_hi[:], in0=turns[:], scalar=-TWO_PI_HI, in1=phase_abs[:], op0=ALU.mult, op1=ALU.add
+        )
+        rest = keep.tile([P, sc], F32)
+        nc.vector.scalar_tensor_tensor(
+            out=rest[:], in0=turns[:], scalar=-TWO_PI_LO, in1=rest_hi[:], op0=ALU.mult, op1=ALU.add
+        )
+        rest_abs = keep.tile([P, sc], F32)
+        nc.scalar.activation(out=rest_abs[:], in_=rest[:], func=ACT.Abs)
+        angle_raw = keep.tile([P, sc], F32)
+        nc.vector.tensor_scalar(
+            out=angle_raw[:], in0=rest_abs[:], scalar1=-1.0, scalar2=math.pi / 2.0, op0=ALU.mult, op1=ALU.add
+        )
+        angle = keep.tile([P, sc], F32)
+        nc.vector.tensor_scalar(out=angle[:], in0=angle_raw[:], scalar1=SIN_FLOOR, scalar2=None, op0=ALU.max)
+        cosine = keep.tile([P, sc], F32)
+        nc.scalar.activation(out=cosine[:], in_=angle[:], func=ACT.Sin)
+        mix = keep.tile([P, sc], F32)
+        nc.vector.tensor_tensor(
+            out=mix[:], in0=amplitudes[:].rearrange("p s c -> p (s c)"), in1=cosine[:], op=ALU.mult
+        )
+        bias_mix = keep.tile([P, sc], F32)
+        nc.vector.tensor_tensor(out=bias_mix[:], in0=bias_t, in1=mix[:], op=ALU.mult)
+
+        x_grouped = keep.tile([P, PASSES, B, PACK], BF16, align_bytes=64)
+        x_codes = keep.tile([P, PASSES, B], U32, align_bytes=64)
+        x_scales = keep.tile([P, PASSES, B], U8, align_bytes=64)
+        words_per_pass = K_PASS // 2
+        for pair in range(ROW_TILES // 2):
+            for g in range(PASSES):
+                turned = bank(2 + PASSES * pair + g, [P, 2, 2, P], F32)
+                for t in range(2):
+                    words = x_rows[:, 2 * pair + t, :].bitcast(F32)
+                    for u in range(2):
+                        nc.tensor.transpose(
+                            turned[:, t, u, :],
+                            words[:, words_per_pass * g + u : words_per_pass * (g + 1) : 2],
+                            ident_f32[:],
+                        )
+                dst = x_grouped[:, g, 2 * P * pair : 2 * P * (pair + 1), :].rearrange("p r j -> p (r j)").bitcast(F32)
+                nc.scalar.copy(
+                    out=dst.rearrange("p (t r u) -> p t r u", t=2, u=2),
+                    in_=turned[:].rearrange("p t u r -> p t r u"),
+                )
+        for g in range(PASSES):
+            nc.vector.quantize_mx(
+                out=x_codes[:, g, :].bitcast(FP8X4),
+                scales=x_scales[:, g, :],
+                in_=x_grouped[:, g, :, :].rearrange("p r j -> p (r j)"),
+            )
+
+        gamma_all = keep.tile([P, Q], BF16)
+        beta_all = keep.tile([P, Q], BF16)
+
+        def load_late_constants():
+            nc.sync.dma_start(out=gamma_all[:], in_=ln_gamma.partition_broadcast(P))
+            nc.sync.dma_start(out=beta_all[:], in_=ln_beta.partition_broadcast(P))
+            for t in range(FOLDED):
+                r = 2 * SPLIT * t
+                nc.sync.dma_start(out=fold_rhs[r : r + SPLIT, t, :], in_=ln_gamma.partition_broadcast(SPLIT))
+                nc.sync.dma_start(
+                    out=fold_rhs[r + SPLIT : r + 2 * SPLIT, t, :], in_=ln_beta.partition_broadcast(SPLIT)
+                )
+
+        w_raw, w_grouped, w_codes, w_scales = {}, {}, {}, {}
+        products, sup_t, scaled_t = {}, {}, {}
+        stat_banks, fold_banks, moments, spread, inv_std, fold_lhs, results = {}, {}, {}, {}, {}, {}, {}
+        split_banks, plain_std = {}, {}
+
+        def piece_place(piece):
+            state, j = divmod(piece, PASSES * HALVES)
+            return state, j % PASSES, j // PASSES
+
+        def load_piece(piece):
+            state, g, half = piece_place(piece)
+            raw = stream.tile([P, PACK, BANK], BF16, bufs=7)
+            rows = W[state, g * K_PASS : (g + 1) * K_PASS, half * BANK : (half + 1) * BANK]
+            nc.sync.dma_start(out=raw[:], in_=rows.rearrange("(p j) n -> p j n", j=PACK))
+            w_raw[piece] = raw
+
+        def interleave(piece, copy, first, last):
+            if piece not in w_grouped:
+                grouped = stream.tile([P, BANK, PACK], BF16, bufs=3, align_bytes=64)
+                w_grouped[piece] = grouped
+            if last > first:
+                copy(
+                    out=w_grouped[piece][:, first:last, :].rearrange("p (c i) j -> p c j i", i=4),
+                    in_=w_raw[piece][:, :, first:last].rearrange("p j (c i) -> p c j i", i=4),
+                )
+
+        def quantize_piece(piece):
+            codes = stream.tile([P, BANK], U32, bufs=7, align_bytes=64)
+            scales = stream.tile([P, BANK], U8, bufs=7, align_bytes=64)
+            nc.vector.quantize_mx(
+                out=codes[:].bitcast(FP8X4), scales=scales[:], in_=w_grouped[piece][:].rearrange("p n j -> p (n j)")
+            )
+            w_codes[piece_place(piece)] = codes
+            w_scales[piece_place(piece)] = scales
+
+        def multiply(state, chunk):
+            half, c = divmod(chunk, CHUNKS_PER_HALF)
+            acc = bank(chunk % 2, [P, B], F32)
+            for g in range(PASSES):
+                nc.tensor.matmul_mx(
+                    out=acc[:],
+                    lhsT=w_codes[state, g, half][:, c * P : (c + 1) * P].bitcast(FP8X4),
+                    lhsT_scale=w_scales[state, g, half][:, c * P : (c + 1) * P],
+                    rhs=x_codes[:, g, :].bitcast(FP8X4),
+                    rhs_scale=x_scales[:, g, :],
+                    start=(g == 0),
+                    stop=(g == PASSES - 1),
+                )
+            products[state, chunk] = acc
+
+        def apply_mix(state, chunk):
+            sup = stream.tile([P, B], F32, bufs=2 * CHUNKS)
+            col = state * CHUNKS + chunk
+            nc.scalar.activation(
+                out=sup[:],
+                in_=products[state, chunk][:],
+                func=ACT.Identity,
+                scale=mix[:, col : col + 1],
+                bias=bias_mix[:, col : col + 1],
+            )
+            sup_t[state, chunk] = sup
+
+        def apply_gamma(state, chunk):
+            scaled = stream.tile([P, FOLDED * P], F32, bufs=3 * CHUNKS)
+            nc.vector.tensor_scalar(
+                out=scaled[:],
+                in0=sup_t[state, chunk][:, 0 : FOLDED * P],
+                scalar1=gamma_t[:, chunk : chunk + 1],
+                scalar2=None,
+                op0=ALU.mult,
+            )
+            scaled_t[state, chunk] = scaled
+
+        def turn_for_stats(state, t):
+            for half in range(HALVES):
+                turned = bank(2 + 2 * (t % 2) + half, [P, BANK], F32)
+                for c in range(CHUNKS_PER_HALF):
+                    nc.tensor.transpose(
+                        turned[:, c * P : (c + 1) * P],
+                        sup_t[state, half * CHUNKS_PER_HALF + c][:, t * P : (t + 1) * P],
+                        ident_f32[:],
+                    )
+                stat_banks[state, t, half] = turned
+
+        def row_moments(state, t):
+            if t == 0:
+                mean_var = stream.tile([P, ROW_TILES, 2], F32, bufs=2)
+                rstd = stream.tile([P, ROW_TILES], F32, bufs=3)
+                moments[state] = mean_var
+                inv_std[state] = rstd
+            partial = stream.tile([P, HALVES, 6], F32, bufs=2)
+            for half in range(HALVES):
+                nc.vector.bn_stats(out=partial[:, half, :], in_=stat_banks[state, t, half][:])
+            nc.vector.bn_aggr(out=moments[state][:, t, :], in_=partial[:].rearrange("p h j -> p (h j)"))
+
+        def folded_std(state):
+            pairs = stream.tile([P, FOLDED, 2], F32, bufs=2)
+            nc.scalar.activation(
+                out=pairs[:, :, 1], in_=moments[state][:, 0:FOLDED, 1], func=ACT.Sqrt, bias=eps[:]
+            )
+            nc.scalar.activation(out=pairs[:, :, 0], in_=moments[state][:, 0:FOLDED, 0], func=ACT.Copy, scale=-1.0)
+            spread[state] = pairs
+
+        def split_moments(state):
+            terms = split_cols[:, 0 : 2 * FOLDED * SPLIT].rearrange("p (v j) -> p v j", j=SPLIT)
+            left = spread[state][:].rearrange("p t w -> p (t w)")
+            for j in range(SPLIT):
+                nc.gpsimd.tensor_copy(out=terms[:, :, j], in_=left)
+                if j + 1 < SPLIT:
+                    remainder = stream.tile([P, 2 * FOLDED], F32, bufs=2)
+                    nc.gpsimd.tensor_tensor(out=remainder[:], in0=left, in1=terms[:, :, j], op=ALU.subtract)
+                    left = remainder[:]
+
+        def turn_split(state):
+            turned = bank(7, [P, P], BF16)
+            nc.tensor.transpose(turned[:], split_cols[:], ident_bf16[:])
+            split_banks[state] = turned
+
+        def fetch_split(state):
+            lhs = stream.tile([P, P], BF16, bufs=2)
+            nc.scalar.copy(out=lhs[:], in_=split_banks[state][:])
+            fold_lhs[state] = lhs
+
+        def turn_and_fold(state, t):
+            for half in range(HALVES):
+                turned = bank(6 + half, [P, BANK], F32)
+                for c in range(CHUNKS_PER_HALF):
+                    nc.tensor.matmul(
+                        out=turned[:, c * P : (c + 1) * P],
+                        lhsT=scaled_t[state, half * CHUNKS_PER_HALF + c][:, t * P : (t + 1) * P],
+                        rhs=ident_f32[:],
+                        start=(c == 0),
+                        stop=False,
+                        is_transpose=True,
+                    )
+                fold_banks[state, t, half] = turned
+            for half in range(HALVES):
+                nc.tensor.matmul(
+                    out=fold_banks[state, t, half][:],
+                    lhsT=fold_lhs[state][:],
+                    rhs=fold_rhs[:, t, half * BANK : (half + 1) * BANK],
+                    start=False,
+                    stop=True,
+                )
+
+        def store(state, t):
+            nc.sync.dma_start(out=out[t * P : (t + 1) * P, state, :], in_=results[state, t][:])
+
+        def finish_folded(state, t):
+            result = stream.tile([P, Q], F32, bufs=5)
+            results[state, t] = result
+            for half in range(HALVES):
+                dst = result[:, half * BANK : (half + 1) * BANK]
+                rstd = inv_std[state][:, t : t + 1]
+                if state == S - 1 and half == 1:
+                    nc.vector.tensor_scalar(
+                        out=dst, in0=fold_banks[state, t, half][:], scalar1=rstd, scalar2=None, op0=ALU.mult
+                    )
+                else:
+                    nc.scalar.activation(out=dst, in_=fold_banks[state, t, half][:], func=ACT.Copy, scale=rstd)
+            store(state, t)
+
+        def centre_plain(state):
+            t = FOLDED
+            result = stream.tile([P, Q], F32, bufs=5)
+            results[state, t] = result
+            for half in range(HALVES):
+                span = slice(half * BANK, (half + 1) * BANK)
+                nc.vector.scalar_tensor_tensor(
+                    out=result[:, span],
+                    in0=stat_banks[state, t, half][:],
+                    scalar=moments[state][:, t, 0:1],
+                    in1=gamma_all[:, span],
+                    op0=ALU.subtract,
+                    op1=ALU.mult,
+                )
+
+        def plain_sqrt(state):
+            std = stream.tile([P, 1], F32, bufs=2)
+            nc.scalar.activation(out=std[:], in_=moments[state][:, FOLDED, 1:2], func=ACT.Sqrt, bias=eps[:])
+            plain_std[state] = std
+
+        def finish_plain(state):
+            t = FOLDED
+            nc.vector.scalar_tensor_tensor(
+                out=results[state, t][:],
+                in0=results[state, t][:],
+                scalar=inv_std[state][:, t : t + 1],
+                in1=beta_all[:],
+                op0=ALU.mult,
+                op1=ALU.add,
+            )
+            store(state, t)
+
+        def live(state):
+            return 0 <= state < S
+
+        with tc.manual_schedule():
+            for step in range(-LOAD_AHEAD, STEPS * (S + 2)):
+                slot, i = divmod(step, STEPS)
+                prev_slot, prev_i = divmod(step - 1, STEPS)
+                if step + LOAD_AHEAD < PIECES:
+                    load_piece(step + LOAD_AHEAD)
+                if step == 0:
+                    load_late_constants()
+                copy_piece = step + COPY_AHEAD
+                copying = 0 <= copy_piece < PIECES
+                cut = vector_columns(step)
+
+                if live(prev_slot - 1):
+                    row_moments(prev_slot - 1, prev_i)
+                if live(prev_slot - 2) and prev_i < FOLDED:
+                    finish_folded(prev_slot - 2, prev_i)
+                if live(slot - 1) and i == FOLDED:
+                    folded_std(slot - 1)
+                    split_moments(slot - 1)
+                if live(slot):
+                    multiply(slot, 2 * i)
+                    multiply(slot, 2 * i + 1)
+                    apply_mix(slot, 2 * i)
+                    apply_mix(slot, 2 * i + 1)
+                if live(slot - 2) and i == 0:
+                    turn_split(slot - 2)
+                    plain_sqrt(slot - 2)
+                    fetch_split(slot - 2)
+                    centre_plain(slot - 2)
+                if live(prev_slot):
+                    apply_gamma(prev_slot, 2 * prev_i)
+                    apply_gamma(prev_slot, 2 * prev_i + 1)
+                if live(slot - 2) and i == 0:
+                    nc.vector.reciprocal(out=inv_std[slot - 2][:, FOLDED:ROW_TILES], in_=plain_std[slot - 2][:])
+                if 0 <= step + QUANT_AHEAD < PIECES:
+                    quantize_piece(step + QUANT_AHEAD)
+                if copying:
+                    interleave(copy_piece, nc.vector.tensor_copy, 0, cut)
+                    interleave(copy_piece, nc.scalar.copy, cut, BANK)
+                if live(slot - 2) and i == 0:
+                    finish_plain(slot - 2)
+                if live(slot - 1) and i == FOLDED:
+                    nc.vector.reciprocal(out=inv_std[slot - 1][:, 0:FOLDED], in_=spread[slot - 1][:, :, 1])
+                if live(slot - 1):
+                    turn_for_stats(slot - 1, i)
+                if live(slot - 2) and i < FOLDED:
+                    turn_and_fold(slot - 2, i)

@@ -27,36 +27,47 @@ HALVES = Q // BANK
 CHUNKS = Q // P
 CHUNKS_PER_HALF = BANK // P
 ROW_TILES = B // P
-FOLDED = ROW_TILES - 1
 SPLIT = 3
 STEPS = ROW_TILES
 PIECES = S * PASSES * HALVES
 LOAD_AHEAD = 8
 COPY_AHEAD = 4
-QUANT_AHEAD = 3
+QUANT_AHEAD = 2
 
+CUT0 = 416
+CUT1 = 208
+CUT2 = 336
+CUT3 = 128
+GAMMA_LAG = 4
+SLOTS = 12
+GV = 1
+LATE = 1
+FOLDS = 33333333
+TAILB = 1
+ORD = 0
+SPLIT_LAG = 2
+RESULT_BUFS = 5
+BK = 1
 TWO_PI_HI = 6.28125
 TWO_PI_LO = 2.0 * math.pi - TWO_PI_HI
 SIN_FLOOR = -3.1415925
 
 
-def vector_columns(step):
-    if step < STEPS:
-        return 368
-    if step < 2 * STEPS:
-        return 176
-    return 0 if step % STEPS == 0 else 320
+def folded(state):
+    return int(str(FOLDS)[state])
 
 
 def tile_quantumsuperposition_kernel(
     tc, language_features, W, b, amplitude_weights, phase_weights, ln_gamma, ln_beta, out
 ):
     nc = tc.nc
+    STAT_BANKS, FOLD_BANKS = ((2, 3, 4), (5, 6, 7)) if BK == 0 else ((2, 3, 4, 5), (6, 7))
 
     with ExitStack() as ctx:
         keep = ctx.enter_context(tc.tile_pool(name="keep", bufs=1))
         stream = ctx.enter_context(tc.tile_pool(name="stream", bufs=2))
         psum = ctx.enter_context(tc.psum_pool(name="psum", bufs=1))
+        ctx.enter_context(tc.manual_schedule())
 
         def bank(index, shape, dtype):
             return psum.tile(shape, dtype, name="bank%d" % index, tag="bank%d" % index)
@@ -87,8 +98,8 @@ def tile_quantumsuperposition_kernel(
 
         split_cols = keep.tile([P, P], BF16)
         nc.gpsimd.memset(split_cols[:], 0.0)
-        fold_rhs = keep.tile([P, FOLDED, Q], BF16)
-        nc.gpsimd.memset(fold_rhs[:], 0.0)
+        fold_rhs = keep.tile([P, ROW_TILES - 1, Q], BF16)
+        nc.vector.memset(fold_rhs[:], 0.0)
 
         cols = bank(6, [P, 2 * P], BF16)
         nc.tensor.transpose(cols[:, 0:P], rows_ap[:], ident_bf16[:])
@@ -101,59 +112,62 @@ def tile_quantumsuperposition_kernel(
         gamma_t = small[:, P + sc : P + sc + CHUNKS]
 
         top = keep.tile([P, 1, CHUNKS], F32)
+        shifted = keep.tile([P, S, CHUNKS], F32)
+        expd = keep.tile([P, S, CHUNKS], F32)
+        total = keep.tile([P, CHUNKS], F32)
+        inv_total = keep.tile([P, 1, CHUNKS], F32)
+        amplitudes = keep.tile([P, S, CHUNKS], F32)
+        phase_abs = keep.tile([P, sc], F32)
+        turns_f = keep.tile([P, sc], F32)
+        turns = keep.tile([P, sc], I32)
+        rest_hi = keep.tile([P, sc], F32)
+        rest = keep.tile([P, sc], F32)
+        rest_neg = keep.tile([P, sc], F32)
+        angle = keep.tile([P, sc], F32)
+        cosine = keep.tile([P, sc], F32)
+        mix = keep.tile([P, sc], F32)
+        bias_mix = keep.tile([P, sc], F32)
         nc.vector.tensor_reduce(
             out=top[:, 0, :], in_=amp_t.rearrange("p (s c) -> p c s", c=CHUNKS), axis=AXIS.X, op=ALU.max
         )
-        shifted = keep.tile([P, S, CHUNKS], F32)
+        nc.vector.scalar_tensor_tensor(
+            out=phase_abs[:], in0=phase_t, scalar=-1.0, in1=phase_t, op0=ALU.mult, op1=ALU.max
+        )
         nc.vector.tensor_tensor(
             out=shifted[:],
             in0=amp_t.rearrange("p (s c) -> p s c", c=CHUNKS),
             in1=top[:].to_broadcast([P, S, CHUNKS]),
             op=ALU.subtract,
         )
-        expd = keep.tile([P, S, CHUNKS], F32)
-        nc.scalar.activation(out=expd[:], in_=shifted[:], func=ACT.Exp)
-        total = keep.tile([P, CHUNKS], F32)
-        nc.vector.tensor_reduce(out=total[:], in_=expd[:].rearrange("p s c -> p c s"), axis=AXIS.X, op=ALU.add)
-        inv_total = keep.tile([P, 1, CHUNKS], F32)
-        nc.vector.reciprocal(out=inv_total[:, 0, :], in_=total[:])
-        amplitudes = keep.tile([P, S, CHUNKS], F32)
-        nc.vector.tensor_tensor(
-            out=amplitudes[:], in0=expd[:], in1=inv_total[:].to_broadcast([P, S, CHUNKS]), op=ALU.mult
-        )
-
-        phase_abs = keep.tile([P, sc], F32)
-        nc.scalar.activation(out=phase_abs[:], in_=phase_t, func=ACT.Abs)
-        turns_f = keep.tile([P, sc], F32)
         nc.vector.tensor_scalar(
             out=turns_f[:], in0=phase_abs[:], scalar1=1.0 / (2.0 * math.pi), scalar2=0.25, op0=ALU.mult, op1=ALU.add
         )
-        turns = keep.tile([P, sc], I32)
+        nc.scalar.activation(out=expd[:], in_=shifted[:], func=ACT.Exp)
         nc.vector.tensor_copy(out=turns[:], in_=turns_f[:])
-        rest_hi = keep.tile([P, sc], F32)
+        nc.vector.tensor_reduce(out=total[:], in_=expd[:].rearrange("p s c -> p c s"), axis=AXIS.X, op=ALU.add)
         nc.vector.scalar_tensor_tensor(
             out=rest_hi[:], in0=turns[:], scalar=-TWO_PI_HI, in1=phase_abs[:], op0=ALU.mult, op1=ALU.add
         )
-        rest = keep.tile([P, sc], F32)
+        nc.vector.reciprocal(out=inv_total[:, 0, :], in_=total[:])
         nc.vector.scalar_tensor_tensor(
             out=rest[:], in0=turns[:], scalar=-TWO_PI_LO, in1=rest_hi[:], op0=ALU.mult, op1=ALU.add
         )
-        rest_abs = keep.tile([P, sc], F32)
-        nc.scalar.activation(out=rest_abs[:], in_=rest[:], func=ACT.Abs)
-        angle_raw = keep.tile([P, sc], F32)
-        nc.vector.tensor_scalar(
-            out=angle_raw[:], in0=rest_abs[:], scalar1=-1.0, scalar2=math.pi / 2.0, op0=ALU.mult, op1=ALU.add
-        )
-        angle = keep.tile([P, sc], F32)
-        nc.vector.tensor_scalar(out=angle[:], in0=angle_raw[:], scalar1=SIN_FLOOR, scalar2=None, op0=ALU.max)
-        cosine = keep.tile([P, sc], F32)
-        nc.scalar.activation(out=cosine[:], in_=angle[:], func=ACT.Sin)
-        mix = keep.tile([P, sc], F32)
         nc.vector.tensor_tensor(
-            out=mix[:], in0=amplitudes[:].rearrange("p s c -> p (s c)"), in1=cosine[:], op=ALU.mult
+            out=amplitudes[:], in0=expd[:], in1=inv_total[:].to_broadcast([P, S, CHUNKS]), op=ALU.mult
         )
-        bias_mix = keep.tile([P, sc], F32)
-        nc.vector.tensor_tensor(out=bias_mix[:], in0=bias_t, in1=mix[:], op=ALU.mult)
+        nc.vector.scalar_tensor_tensor(out=rest_neg[:], in0=rest[:], scalar=-1.0, in1=rest[:], op0=ALU.mult, op1=ALU.min)
+        nc.vector.tensor_scalar(
+            out=angle[:], in0=rest_neg[:], scalar1=math.pi / 2.0, scalar2=SIN_FLOOR, op0=ALU.add, op1=ALU.max
+        )
+        nc.scalar.activation(out=cosine[:], in_=angle[:], func=ACT.Sin)
+
+        def mix_weights():
+            nc.vector.tensor_tensor(
+                out=mix[:], in0=amplitudes[:].rearrange("p s c -> p (s c)"), in1=cosine[:], op=ALU.mult
+            )
+
+        def mix_bias():
+            nc.vector.tensor_tensor(out=bias_mix[:], in0=bias_t, in1=mix[:], op=ALU.mult)
 
         x_grouped = keep.tile([P, PASSES, B, PACK], BF16, align_bytes=64)
         x_codes = keep.tile([P, PASSES, B], U32, align_bytes=64)
@@ -175,7 +189,8 @@ def tile_quantumsuperposition_kernel(
                     out=dst.rearrange("p (t r u) -> p t r u", t=2, u=2),
                     in_=turned[:].rearrange("p t u r -> p t r u"),
                 )
-        for g in range(PASSES):
+
+        def quantize_features(g):
             nc.vector.quantize_mx(
                 out=x_codes[:, g, :].bitcast(FP8X4),
                 scales=x_scales[:, g, :],
@@ -188,7 +203,7 @@ def tile_quantumsuperposition_kernel(
         def load_late_constants():
             nc.sync.dma_start(out=gamma_all[:], in_=ln_gamma.partition_broadcast(P))
             nc.sync.dma_start(out=beta_all[:], in_=ln_beta.partition_broadcast(P))
-            for t in range(FOLDED):
+            for t in range(ROW_TILES - 1):
                 r = 2 * SPLIT * t
                 nc.sync.dma_start(out=fold_rhs[r : r + SPLIT, t, :], in_=ln_gamma.partition_broadcast(SPLIT))
                 nc.sync.dma_start(
@@ -198,11 +213,15 @@ def tile_quantumsuperposition_kernel(
         w_raw, w_grouped, w_codes, w_scales = {}, {}, {}, {}
         products, sup_t, scaled_t = {}, {}, {}
         stat_banks, fold_banks, moments, spread, inv_std, fold_lhs, results = {}, {}, {}, {}, {}, {}, {}
-        split_banks, plain_std = {}, {}
+        partials, fold_turns = {}, []
 
         def piece_place(piece):
             state, j = divmod(piece, PASSES * HALVES)
             return state, j % PASSES, j // PASSES
+
+        def shared_slot(piece, shape, dtype):
+            name = "slot%d" % (piece % SLOTS)
+            return keep.tile(shape, dtype, name=name, tag=name, align_bytes=64)
 
         def load_piece(piece):
             state, g, half = piece_place(piece)
@@ -213,7 +232,7 @@ def tile_quantumsuperposition_kernel(
 
         def interleave(piece, copy, first, last):
             if piece not in w_grouped:
-                grouped = stream.tile([P, BANK, PACK], BF16, bufs=3, align_bytes=64)
+                grouped = shared_slot(piece, [P, BANK, PACK], BF16)
                 w_grouped[piece] = grouped
             if last > first:
                 copy(
@@ -257,20 +276,24 @@ def tile_quantumsuperposition_kernel(
             )
             sup_t[state, chunk] = sup
 
-        def apply_gamma(state, chunk):
-            scaled = stream.tile([P, FOLDED * P], F32, bufs=3 * CHUNKS)
-            nc.vector.tensor_scalar(
-                out=scaled[:],
-                in0=sup_t[state, chunk][:, 0 : FOLDED * P],
-                scalar1=gamma_t[:, chunk : chunk + 1],
-                scalar2=None,
-                op0=ALU.mult,
-            )
-            scaled_t[state, chunk] = scaled
+        def apply_gamma(state, pair, piece):
+            width = folded(state) * P
+            scaled = shared_slot(piece, [P, 2, B], F32)
+            for j in range(2):
+                chunk = 2 * pair + j
+                (nc.gpsimd if GV else nc.vector).tensor_scalar(
+                    out=scaled[:, j, 0:width],
+                    in0=sup_t[state, chunk][:, 0:width],
+                    scalar1=gamma_t[:, chunk : chunk + 1],
+                    scalar2=0.0,
+                    op0=ALU.mult,
+                    op1=ALU.add,
+                )
+                scaled_t[state, chunk] = scaled[:, j, :]
 
         def turn_for_stats(state, t):
             for half in range(HALVES):
-                turned = bank(2 + 2 * (t % 2) + half, [P, BANK], F32)
+                turned = bank(STAT_BANKS[len(stat_banks) % len(STAT_BANKS)], [P, BANK], F32)
                 for c in range(CHUNKS_PER_HALF):
                     nc.tensor.transpose(
                         turned[:, c * P : (c + 1) * P],
@@ -279,48 +302,62 @@ def tile_quantumsuperposition_kernel(
                     )
                 stat_banks[state, t, half] = turned
 
-        def row_moments(state, t):
+        def row_partials(state, t):
             if t == 0:
                 mean_var = stream.tile([P, ROW_TILES, 2], F32, bufs=2)
+                pairs = stream.tile([P, ROW_TILES, 2], F32, bufs=2)
                 rstd = stream.tile([P, ROW_TILES], F32, bufs=3)
                 moments[state] = mean_var
+                spread[state] = pairs
                 inv_std[state] = rstd
             partial = stream.tile([P, HALVES, 6], F32, bufs=2)
             for half in range(HALVES):
                 nc.vector.bn_stats(out=partial[:, half, :], in_=stat_banks[state, t, half][:])
-            nc.vector.bn_aggr(out=moments[state][:, t, :], in_=partial[:].rearrange("p h j -> p (h j)"))
+            partials[state, t] = partial
 
-        def folded_std(state):
-            pairs = stream.tile([P, FOLDED, 2], F32, bufs=2)
+        def row_moments(state, t):
+            nc.vector.bn_aggr(out=moments[state][:, t, :], in_=partials[state, t][:].rearrange("p h j -> p (h j)"))
+
+        def row_std(state, first, last):
             nc.scalar.activation(
-                out=pairs[:, :, 1], in_=moments[state][:, 0:FOLDED, 1], func=ACT.Sqrt, bias=eps[:]
+                out=spread[state][:, first:last, 1], in_=moments[state][:, first:last, 1], func=ACT.Sqrt, bias=eps[:]
             )
-            nc.scalar.activation(out=pairs[:, :, 0], in_=moments[state][:, 0:FOLDED, 0], func=ACT.Copy, scale=-1.0)
-            spread[state] = pairs
+
+        def row_rstd(state, first, last):
+            nc.vector.reciprocal(out=inv_std[state][:, first:last], in_=spread[state][:, first:last, 1])
+
+        def negate_means(state):
+            count = folded(state)
+            nc.scalar.activation(
+                out=spread[state][:, 0:count, 0], in_=moments[state][:, 0:count, 0], func=ACT.Copy, scale=-1.0
+            )
 
         def split_moments(state):
-            terms = split_cols[:, 0 : 2 * FOLDED * SPLIT].rearrange("p (v j) -> p v j", j=SPLIT)
-            left = spread[state][:].rearrange("p t w -> p (t w)")
+            count = folded(state)
+            terms = split_cols[:, 0 : 2 * count * SPLIT].rearrange("p (v j) -> p v j", j=SPLIT)
+            left = spread[state][:, 0:count, :].rearrange("p t w -> p (t w)")
             for j in range(SPLIT):
                 nc.gpsimd.tensor_copy(out=terms[:, :, j], in_=left)
                 if j + 1 < SPLIT:
-                    remainder = stream.tile([P, 2 * FOLDED], F32, bufs=2)
+                    remainder = stream.tile([P, 2 * count], F32, bufs=2)
                     nc.gpsimd.tensor_tensor(out=remainder[:], in0=left, in1=terms[:, :, j], op=ALU.subtract)
                     left = remainder[:]
 
-        def turn_split(state):
-            turned = bank(7, [P, P], BF16)
-            nc.tensor.transpose(turned[:], split_cols[:], ident_bf16[:])
-            split_banks[state] = turned
+        def next_fold_bank(shape, dtype):
+            fold_turns.append(len(fold_turns))
+            ring = FOLD_BANKS + (0, 1) if TAILB and len(products) == S * CHUNKS else FOLD_BANKS
+            return bank(ring[fold_turns[-1] % len(ring)], shape, dtype)
 
-        def fetch_split(state):
+        def turn_split(state):
+            turned = next_fold_bank([P, P], BF16)
+            nc.tensor.transpose(turned[:], split_cols[:], ident_bf16[:])
             lhs = stream.tile([P, P], BF16, bufs=2)
-            nc.scalar.copy(out=lhs[:], in_=split_banks[state][:])
+            nc.scalar.copy(out=lhs[:], in_=turned[:])
             fold_lhs[state] = lhs
 
         def turn_and_fold(state, t):
             for half in range(HALVES):
-                turned = bank(6 + half, [P, BANK], F32)
+                turned = next_fold_bank([P, BANK], F32)
                 for c in range(CHUNKS_PER_HALF):
                     nc.tensor.matmul(
                         out=turned[:, c * P : (c + 1) * P],
@@ -344,22 +381,20 @@ def tile_quantumsuperposition_kernel(
             nc.sync.dma_start(out=out[t * P : (t + 1) * P, state, :], in_=results[state, t][:])
 
         def finish_folded(state, t):
-            result = stream.tile([P, Q], F32, bufs=5)
+            result = stream.tile([P, Q], F32, bufs=RESULT_BUFS)
             results[state, t] = result
+            rstd = inv_std[state][:, t : t + 1]
             for half in range(HALVES):
                 dst = result[:, half * BANK : (half + 1) * BANK]
-                rstd = inv_std[state][:, t : t + 1]
+                src = fold_banks[state, t, half][:]
                 if state == S - 1 and half == 1:
-                    nc.vector.tensor_scalar(
-                        out=dst, in0=fold_banks[state, t, half][:], scalar1=rstd, scalar2=None, op0=ALU.mult
-                    )
+                    nc.vector.tensor_scalar(out=dst, in0=src, scalar1=rstd, scalar2=None, op0=ALU.mult)
                 else:
-                    nc.scalar.activation(out=dst, in_=fold_banks[state, t, half][:], func=ACT.Copy, scale=rstd)
+                    nc.scalar.activation(out=dst, in_=src, func=ACT.Copy, scale=rstd)
             store(state, t)
 
-        def centre_plain(state):
-            t = FOLDED
-            result = stream.tile([P, Q], F32, bufs=5)
+        def centre_plain(state, t):
+            result = stream.tile([P, Q], F32, bufs=RESULT_BUFS)
             results[state, t] = result
             for half in range(HALVES):
                 span = slice(half * BANK, (half + 1) * BANK)
@@ -372,13 +407,7 @@ def tile_quantumsuperposition_kernel(
                     op1=ALU.mult,
                 )
 
-        def plain_sqrt(state):
-            std = stream.tile([P, 1], F32, bufs=2)
-            nc.scalar.activation(out=std[:], in_=moments[state][:, FOLDED, 1:2], func=ACT.Sqrt, bias=eps[:])
-            plain_std[state] = std
-
-        def finish_plain(state):
-            t = FOLDED
+        def finish_plain(state, t):
             nc.vector.scalar_tensor_tensor(
                 out=results[state, t][:],
                 in0=results[state, t][:],
@@ -389,53 +418,86 @@ def tile_quantumsuperposition_kernel(
             )
             store(state, t)
 
-        def live(state):
-            return 0 <= state < S
+        tiles = [(state, t) for state in range(S) for t in range(ROW_TILES)]
+        turn_step = {(state, t): STEPS * (state + 1) + t for state, t in tiles}
+        split_step = {state: turn_step[state, folded(state) - 1] + 1 for state in range(S) if folded(state)}
+        fold_step = {(state, t): split_step[state] + SPLIT_LAG + 1 + t for state, t in tiles if t < folded(state)}
+        last_step = max(max(fold_step.values()) + 1, max(turn_step.values()) + 2)
 
-        with tc.manual_schedule():
-            for step in range(-LOAD_AHEAD, STEPS * (S + 2)):
-                slot, i = divmod(step, STEPS)
-                prev_slot, prev_i = divmod(step - 1, STEPS)
-                if step + LOAD_AHEAD < PIECES:
-                    load_piece(step + LOAD_AHEAD)
-                if step == 0:
-                    load_late_constants()
-                copy_piece = step + COPY_AHEAD
-                copying = 0 <= copy_piece < PIECES
-                cut = vector_columns(step)
+        def due(table, step):
+            return [key for key in table if table[key] == step]
 
-                if live(prev_slot - 1):
-                    row_moments(prev_slot - 1, prev_i)
-                if live(prev_slot - 2) and prev_i < FOLDED:
-                    finish_folded(prev_slot - 2, prev_i)
-                if live(slot - 1) and i == FOLDED:
-                    folded_std(slot - 1)
-                    split_moments(slot - 1)
-                if live(slot):
-                    multiply(slot, 2 * i)
-                    multiply(slot, 2 * i + 1)
-                    apply_mix(slot, 2 * i)
-                    apply_mix(slot, 2 * i + 1)
-                if live(slot - 2) and i == 0:
-                    turn_split(slot - 2)
-                    plain_sqrt(slot - 2)
-                    fetch_split(slot - 2)
-                    centre_plain(slot - 2)
-                if live(prev_slot):
-                    apply_gamma(prev_slot, 2 * prev_i)
-                    apply_gamma(prev_slot, 2 * prev_i + 1)
-                if live(slot - 2) and i == 0:
-                    nc.vector.reciprocal(out=inv_std[slot - 2][:, FOLDED:ROW_TILES], in_=plain_std[slot - 2][:])
-                if 0 <= step + QUANT_AHEAD < PIECES:
-                    quantize_piece(step + QUANT_AHEAD)
-                if copying:
-                    interleave(copy_piece, nc.vector.tensor_copy, 0, cut)
-                    interleave(copy_piece, nc.scalar.copy, cut, BANK)
-                if live(slot - 2) and i == 0:
-                    finish_plain(slot - 2)
-                if live(slot - 1) and i == FOLDED:
-                    nc.vector.reciprocal(out=inv_std[slot - 1][:, 0:FOLDED], in_=spread[slot - 1][:, :, 1])
-                if live(slot - 1):
-                    turn_for_stats(slot - 1, i)
-                if live(slot - 2) and i < FOLDED:
-                    turn_and_fold(slot - 2, i)
+        for step in range(-LOAD_AHEAD, last_step + 1):
+            slot, i = divmod(step, STEPS)
+            if step + LOAD_AHEAD < PIECES:
+                load_piece(step + LOAD_AHEAD)
+            if step == 0:
+                load_late_constants()
+            copy_piece = step + COPY_AHEAD
+            copying = 0 <= copy_piece < PIECES
+            measured = due(turn_step, step - 1)
+            plain = [(state, t) for state, t in measured if t >= folded(state)]
+
+            closing = [(state, t) for state, t in due(turn_step, step - 2) if t >= folded(state)]
+            if copy_piece < 2:
+                cut = BANK
+            elif copy_piece == 2:
+                cut = 0
+            elif not measured:
+                cut = CUT0
+            else:
+                cut = (CUT2 if due(fold_step, step - 1) else CUT1) - CUT3 * (len(plain) + len(closing))
+            if step + QUANT_AHEAD == 0:
+                mix_weights()
+            if 0 <= step + QUANT_AHEAD < PIECES:
+                quantize_piece(step + QUANT_AHEAD)
+            if step + QUANT_AHEAD == 0:
+                quantize_features(0)
+                mix_bias()
+                quantize_features(1)
+            gslot, gi = divmod(step - GAMMA_LAG, STEPS)
+            if 0 <= gslot < S and folded(gslot):
+                apply_gamma(gslot, gi, step + QUANT_AHEAD)
+            for state in due(split_step, step - 1):
+                if LATE:
+                    split_moments(state)
+            for state, t in measured:
+                row_partials(state, t)
+            for state, t in due(fold_step, step - 1):
+                finish_folded(state, t)
+            if 0 <= slot < S:
+                for chunk in (2 * i, 2 * i + 1):
+                    multiply(slot, chunk)
+                for chunk in (2 * i, 2 * i + 1):
+                    apply_mix(slot, chunk)
+            for state, t in due(turn_step, step - 2):
+                if t >= folded(state):
+                    row_rstd(state, t, t + 1)
+            for state in due(split_step, step - 1):
+                row_rstd(state, 0, folded(state))
+            if copying and not ORD:
+                interleave(copy_piece, nc.vector.tensor_copy, 0, cut)
+            for state, t in measured:
+                row_moments(state, t)
+            if copying and ORD:
+                interleave(copy_piece, nc.vector.tensor_copy, 0, cut)
+            for state, t in due(turn_step, step - 2):
+                if t >= folded(state):
+                    finish_plain(state, t)
+            for state, t in plain:
+                centre_plain(state, t)
+            if copying:
+                interleave(copy_piece, nc.scalar.copy, cut, BANK)
+            for state in due(split_step, step):
+                row_std(state, 0, folded(state))
+                negate_means(state)
+                if not LATE:
+                    split_moments(state)
+            for state, t in plain:
+                row_std(state, t, t + 1)
+            for state, t in due(turn_step, step):
+                turn_for_stats(state, t)
+            for state in due(split_step, step - SPLIT_LAG):
+                turn_split(state)
+            for state, t in due(fold_step, step):
+                turn_and_fold(state, t)

@@ -27,41 +27,42 @@ HALVES = Q // BANK
 CHUNKS = Q // P
 CHUNKS_PER_HALF = BANK // P
 ROW_TILES = B // P
-SPLIT = 3
+FOLDED = ROW_TILES - 1
+PLAIN = ROW_TILES - 1
+TERMS = 3
+GROUP = 4
+
 STEPS = ROW_TILES
 PIECES = S * PASSES * HALVES
 LOAD_AHEAD = 8
 COPY_AHEAD = 4
 QUANT_AHEAD = 2
-
-CUT0 = 416
-CUT1 = 208
-CUT2 = 336
-CUT3 = 128
-GAMMA_LAG = 4
-SLOTS = 12
-GV = 1
-LATE = 1
-FOLDS = 33333333
-TAILB = 1
-ORD = 0
+GAMMA_LAG = 5
 SPLIT_LAG = 2
+
+RING = 11
+RAW_BUFS = 7
+CODE_BUFS = 7
 RESULT_BUFS = 5
-BK = 1
+
+PRODUCT_BANKS = (0, 1)
+STAT_BANKS = (2, 3, 4, 5)
+FOLD_BANKS = (6, 7)
+
+SHARE_NO_STATS = 416
+SHARE_NO_FINISH = 224
+SHARE_FINISH = 352
+SHARE_PLAIN_COST = 112
+
 TWO_PI_HI = 6.28125
 TWO_PI_LO = 2.0 * math.pi - TWO_PI_HI
 SIN_FLOOR = -3.1415925
-
-
-def folded(state):
-    return int(str(FOLDS)[state])
 
 
 def tile_quantumsuperposition_kernel(
     tc, language_features, W, b, amplitude_weights, phase_weights, ln_gamma, ln_beta, out
 ):
     nc = tc.nc
-    STAT_BANKS, FOLD_BANKS = ((2, 3, 4), (5, 6, 7)) if BK == 0 else ((2, 3, 4, 5), (6, 7))
 
     with ExitStack() as ctx:
         keep = ctx.enter_context(tc.tile_pool(name="keep", bufs=1))
@@ -77,14 +78,17 @@ def tile_quantumsuperposition_kernel(
         make_identity(nc, ident_bf16[:])
         make_identity(nc, ident_f32[:])
 
-        rows_ap = keep.tile([P, P], BF16)
-        rows_bg = keep.tile([P, P], BF16)
-        sc = S * CHUNKS
-        nc.vector.memset(rows_bg[:], 0.0)
-        nc.scalar.dma_start(out=rows_ap[0:sc, :], in_=amplitude_weights.rearrange("s (c p) -> (s c) p", p=P))
-        nc.scalar.dma_start(out=rows_ap[sc:P, :], in_=phase_weights.rearrange("s (c p) -> (s c) p", p=P))
-        nc.scalar.dma_start(out=rows_bg[0:sc, :], in_=b.rearrange("s (c p) -> (s c) p", p=P))
-        nc.scalar.dma_start(out=rows_bg[sc : sc + CHUNKS, :], in_=ln_gamma.rearrange("(c p) -> c p", p=P))
+        per_state = S * CHUNKS
+        rows_amp_phase = keep.tile([P, P], BF16)
+        rows_bias_gamma = keep.tile([P, P], BF16)
+        nc.vector.memset(rows_bias_gamma[:], 0.0)
+        as_rows = "s (c p) -> (s c) p"
+        nc.scalar.dma_start(out=rows_amp_phase[0:per_state, :], in_=amplitude_weights.rearrange(as_rows, p=P))
+        nc.scalar.dma_start(out=rows_amp_phase[per_state:P, :], in_=phase_weights.rearrange(as_rows, p=P))
+        nc.scalar.dma_start(out=rows_bias_gamma[0:per_state, :], in_=b.rearrange(as_rows, p=P))
+        nc.scalar.dma_start(
+            out=rows_bias_gamma[per_state : per_state + CHUNKS, :], in_=ln_gamma.rearrange("(c p) -> c p", p=P)
+        )
 
         x_rows = keep.tile([P, ROW_TILES, I], BF16)
         x_hbm = language_features.rearrange("(t p) k -> p t k", p=P)
@@ -96,20 +100,20 @@ def tile_quantumsuperposition_kernel(
         nc.vector.memset(one[:], 1.0)
         nc.vector.tensor_scalar(out=eps[:], in0=one[:], scalar1=LN_EPS, scalar2=None, op0=ALU.mult)
 
-        split_cols = keep.tile([P, P], BF16)
-        nc.gpsimd.memset(split_cols[:], 0.0)
-        fold_rhs = keep.tile([P, ROW_TILES - 1, Q], BF16)
+        term_cols = keep.tile([P, P], BF16)
+        nc.gpsimd.memset(term_cols[:], 0.0)
+        fold_rhs = keep.tile([P, FOLDED, Q], BF16)
         nc.vector.memset(fold_rhs[:], 0.0)
 
-        cols = bank(6, [P, 2 * P], BF16)
-        nc.tensor.transpose(cols[:, 0:P], rows_ap[:], ident_bf16[:])
-        nc.tensor.transpose(cols[:, P : 2 * P], rows_bg[:], ident_bf16[:])
+        small_turned = bank(FOLD_BANKS[0], [P, 2 * P], BF16)
+        nc.tensor.transpose(small_turned[:, 0:P], rows_amp_phase[:], ident_bf16[:])
+        nc.tensor.transpose(small_turned[:, P : 2 * P], rows_bias_gamma[:], ident_bf16[:])
         small = keep.tile([P, 2 * P], F32)
-        nc.vector.tensor_copy(out=small[:], in_=cols[:])
-        amp_t = small[:, 0:sc]
-        phase_t = small[:, sc:P]
-        bias_t = small[:, P : P + sc]
-        gamma_t = small[:, P + sc : P + sc + CHUNKS]
+        nc.vector.tensor_copy(out=small[:], in_=small_turned[:])
+        amp_cm = small[:, 0:per_state]
+        phase_cm = small[:, per_state:P]
+        bias_cm = small[:, P : P + per_state]
+        gamma_cm = small[:, P + per_state : P + per_state + CHUNKS]
 
         top = keep.tile([P, 1, CHUNKS], F32)
         shifted = keep.tile([P, S, CHUNKS], F32)
@@ -117,33 +121,33 @@ def tile_quantumsuperposition_kernel(
         total = keep.tile([P, CHUNKS], F32)
         inv_total = keep.tile([P, 1, CHUNKS], F32)
         amplitudes = keep.tile([P, S, CHUNKS], F32)
-        phase_abs = keep.tile([P, sc], F32)
-        turns_f = keep.tile([P, sc], F32)
-        turns = keep.tile([P, sc], I32)
-        rest_hi = keep.tile([P, sc], F32)
-        rest = keep.tile([P, sc], F32)
-        rest_neg = keep.tile([P, sc], F32)
-        angle = keep.tile([P, sc], F32)
-        cosine = keep.tile([P, sc], F32)
-        mix = keep.tile([P, sc], F32)
-        bias_mix = keep.tile([P, sc], F32)
+        phase_abs = keep.tile([P, per_state], F32)
+        turns_f32 = keep.tile([P, per_state], F32)
+        turns = keep.tile([P, per_state], I32)
+        rest_hi = keep.tile([P, per_state], F32)
+        rest = keep.tile([P, per_state], F32)
+        rest_neg_abs = keep.tile([P, per_state], F32)
+        angle = keep.tile([P, per_state], F32)
+        cosine = keep.tile([P, per_state], F32)
+        mix = keep.tile([P, per_state], F32)
+        bias_mix = keep.tile([P, per_state], F32)
         nc.vector.tensor_reduce(
-            out=top[:, 0, :], in_=amp_t.rearrange("p (s c) -> p c s", c=CHUNKS), axis=AXIS.X, op=ALU.max
+            out=top[:, 0, :], in_=amp_cm.rearrange("p (s c) -> p c s", c=CHUNKS), axis=AXIS.X, op=ALU.max
         )
         nc.vector.scalar_tensor_tensor(
-            out=phase_abs[:], in0=phase_t, scalar=-1.0, in1=phase_t, op0=ALU.mult, op1=ALU.max
+            out=phase_abs[:], in0=phase_cm, scalar=-1.0, in1=phase_cm, op0=ALU.mult, op1=ALU.max
         )
         nc.vector.tensor_tensor(
             out=shifted[:],
-            in0=amp_t.rearrange("p (s c) -> p s c", c=CHUNKS),
+            in0=amp_cm.rearrange("p (s c) -> p s c", c=CHUNKS),
             in1=top[:].to_broadcast([P, S, CHUNKS]),
             op=ALU.subtract,
         )
         nc.vector.tensor_scalar(
-            out=turns_f[:], in0=phase_abs[:], scalar1=1.0 / (2.0 * math.pi), scalar2=0.25, op0=ALU.mult, op1=ALU.add
+            out=turns_f32[:], in0=phase_abs[:], scalar1=1.0 / (2.0 * math.pi), scalar2=0.25, op0=ALU.mult, op1=ALU.add
         )
         nc.scalar.activation(out=expd[:], in_=shifted[:], func=ACT.Exp)
-        nc.vector.tensor_copy(out=turns[:], in_=turns_f[:])
+        nc.vector.tensor_copy(out=turns[:], in_=turns_f32[:])
         nc.vector.tensor_reduce(out=total[:], in_=expd[:].rearrange("p s c -> p c s"), axis=AXIS.X, op=ALU.add)
         nc.vector.scalar_tensor_tensor(
             out=rest_hi[:], in0=turns[:], scalar=-TWO_PI_HI, in1=phase_abs[:], op0=ALU.mult, op1=ALU.add
@@ -155,19 +159,21 @@ def tile_quantumsuperposition_kernel(
         nc.vector.tensor_tensor(
             out=amplitudes[:], in0=expd[:], in1=inv_total[:].to_broadcast([P, S, CHUNKS]), op=ALU.mult
         )
-        nc.vector.scalar_tensor_tensor(out=rest_neg[:], in0=rest[:], scalar=-1.0, in1=rest[:], op0=ALU.mult, op1=ALU.min)
+        nc.vector.scalar_tensor_tensor(
+            out=rest_neg_abs[:], in0=rest[:], scalar=-1.0, in1=rest[:], op0=ALU.mult, op1=ALU.min
+        )
         nc.vector.tensor_scalar(
-            out=angle[:], in0=rest_neg[:], scalar1=math.pi / 2.0, scalar2=SIN_FLOOR, op0=ALU.add, op1=ALU.max
+            out=angle[:], in0=rest_neg_abs[:], scalar1=math.pi / 2.0, scalar2=SIN_FLOOR, op0=ALU.add, op1=ALU.max
         )
         nc.scalar.activation(out=cosine[:], in_=angle[:], func=ACT.Sin)
 
-        def mix_weights():
+        def make_mix():
             nc.vector.tensor_tensor(
                 out=mix[:], in0=amplitudes[:].rearrange("p s c -> p (s c)"), in1=cosine[:], op=ALU.mult
             )
 
-        def mix_bias():
-            nc.vector.tensor_tensor(out=bias_mix[:], in0=bias_t, in1=mix[:], op=ALU.mult)
+        def make_bias_mix():
+            nc.vector.tensor_tensor(out=bias_mix[:], in0=bias_cm, in1=mix[:], op=ALU.mult)
 
         x_grouped = keep.tile([P, PASSES, B, PACK], BF16, align_bytes=64)
         x_codes = keep.tile([P, PASSES, B], U32, align_bytes=64)
@@ -175,19 +181,19 @@ def tile_quantumsuperposition_kernel(
         words_per_pass = K_PASS // 2
         for pair in range(ROW_TILES // 2):
             for g in range(PASSES):
-                turned = bank(2 + PASSES * pair + g, [P, 2, 2, P], F32)
+                x_turned = bank(STAT_BANKS[PASSES * pair + g], [P, 2, 2, P], F32)
                 for t in range(2):
                     words = x_rows[:, 2 * pair + t, :].bitcast(F32)
                     for u in range(2):
                         nc.tensor.transpose(
-                            turned[:, t, u, :],
+                            x_turned[:, t, u, :],
                             words[:, words_per_pass * g + u : words_per_pass * (g + 1) : 2],
                             ident_f32[:],
                         )
                 dst = x_grouped[:, g, 2 * P * pair : 2 * P * (pair + 1), :].rearrange("p r j -> p (r j)").bitcast(F32)
                 nc.scalar.copy(
                     out=dst.rearrange("p (t r u) -> p t r u", t=2, u=2),
-                    in_=turned[:].rearrange("p t u r -> p t r u"),
+                    in_=x_turned[:].rearrange("p t u r -> p t r u"),
                 )
 
         def quantize_features(g):
@@ -200,49 +206,49 @@ def tile_quantumsuperposition_kernel(
         gamma_all = keep.tile([P, Q], BF16)
         beta_all = keep.tile([P, Q], BF16)
 
-        def load_late_constants():
+        def load_norm_vectors():
             nc.sync.dma_start(out=gamma_all[:], in_=ln_gamma.partition_broadcast(P))
             nc.sync.dma_start(out=beta_all[:], in_=ln_beta.partition_broadcast(P))
-            for t in range(ROW_TILES - 1):
-                r = 2 * SPLIT * t
-                nc.sync.dma_start(out=fold_rhs[r : r + SPLIT, t, :], in_=ln_gamma.partition_broadcast(SPLIT))
+            for t in range(FOLDED):
+                row = 2 * TERMS * t
+                nc.sync.dma_start(out=fold_rhs[row : row + TERMS, t, :], in_=ln_gamma.partition_broadcast(TERMS))
                 nc.sync.dma_start(
-                    out=fold_rhs[r + SPLIT : r + 2 * SPLIT, t, :], in_=ln_beta.partition_broadcast(SPLIT)
+                    out=fold_rhs[row + TERMS : row + 2 * TERMS, t, :], in_=ln_beta.partition_broadcast(TERMS)
                 )
 
         w_raw, w_grouped, w_codes, w_scales = {}, {}, {}, {}
-        products, sup_t, scaled_t = {}, {}, {}
-        stat_banks, fold_banks, moments, spread, inv_std, fold_lhs, results = {}, {}, {}, {}, {}, {}, {}
-        partials, fold_turns = {}, []
+        products, sup_cm, scaled_cm = {}, {}, {}
+        stat_tiles, partials, moments, neg_mean_std, inv_std = {}, {}, {}, {}, {}
+        fold_lhs, fold_tiles, results = {}, {}, {}
+        fold_turns = []
 
         def piece_place(piece):
             state, j = divmod(piece, PASSES * HALVES)
             return state, j % PASSES, j // PASSES
 
-        def shared_slot(piece, shape, dtype):
-            name = "slot%d" % (piece % SLOTS)
+        def ring_tile(piece, shape, dtype):
+            name = "ring%d" % (piece % RING)
             return keep.tile(shape, dtype, name=name, tag=name, align_bytes=64)
 
         def load_piece(piece):
             state, g, half = piece_place(piece)
-            raw = stream.tile([P, PACK, BANK], BF16, bufs=7)
+            raw = stream.tile([P, PACK, BANK], BF16, bufs=RAW_BUFS)
             rows = W[state, g * K_PASS : (g + 1) * K_PASS, half * BANK : (half + 1) * BANK]
             nc.sync.dma_start(out=raw[:], in_=rows.rearrange("(p j) n -> p j n", j=PACK))
             w_raw[piece] = raw
 
         def interleave(piece, copy, first, last):
             if piece not in w_grouped:
-                grouped = shared_slot(piece, [P, BANK, PACK], BF16)
-                w_grouped[piece] = grouped
+                w_grouped[piece] = ring_tile(piece, [P, BANK, PACK], BF16)
             if last > first:
                 copy(
-                    out=w_grouped[piece][:, first:last, :].rearrange("p (c i) j -> p c j i", i=4),
-                    in_=w_raw[piece][:, :, first:last].rearrange("p j (c i) -> p c j i", i=4),
+                    out=w_grouped[piece][:, first:last, :].rearrange("p (c i) j -> p c j i", i=GROUP),
+                    in_=w_raw[piece][:, :, first:last].rearrange("p j (c i) -> p c j i", i=GROUP),
                 )
 
         def quantize_piece(piece):
-            codes = stream.tile([P, BANK], U32, bufs=7, align_bytes=64)
-            scales = stream.tile([P, BANK], U8, bufs=7, align_bytes=64)
+            codes = stream.tile([P, BANK], U32, bufs=CODE_BUFS, align_bytes=64)
+            scales = stream.tile([P, BANK], U8, bufs=CODE_BUFS, align_bytes=64)
             nc.vector.quantize_mx(
                 out=codes[:].bitcast(FP8X4), scales=scales[:], in_=w_grouped[piece][:].rearrange("p n j -> p (n j)")
             )
@@ -251,7 +257,7 @@ def tile_quantumsuperposition_kernel(
 
         def multiply(state, chunk):
             half, c = divmod(chunk, CHUNKS_PER_HALF)
-            acc = bank(chunk % 2, [P, B], F32)
+            acc = bank(PRODUCT_BANKS[chunk % len(PRODUCT_BANKS)], [P, B], F32)
             for g in range(PASSES):
                 nc.tensor.matmul_mx(
                     out=acc[:],
@@ -274,45 +280,44 @@ def tile_quantumsuperposition_kernel(
                 scale=mix[:, col : col + 1],
                 bias=bias_mix[:, col : col + 1],
             )
-            sup_t[state, chunk] = sup
+            sup_cm[state, chunk] = sup
 
         def apply_gamma(state, pair, piece):
-            width = folded(state) * P
-            scaled = shared_slot(piece, [P, 2, B], F32)
+            scaled = ring_tile(piece, [P, 2, B], F32)
             for j in range(2):
                 chunk = 2 * pair + j
-                (nc.gpsimd if GV else nc.vector).tensor_scalar(
-                    out=scaled[:, j, 0:width],
-                    in0=sup_t[state, chunk][:, 0:width],
-                    scalar1=gamma_t[:, chunk : chunk + 1],
+                nc.gpsimd.tensor_scalar(
+                    out=scaled[:, j, 0 : FOLDED * P],
+                    in0=sup_cm[state, chunk][:, 0 : FOLDED * P],
+                    scalar1=gamma_cm[:, chunk : chunk + 1],
                     scalar2=0.0,
                     op0=ALU.mult,
                     op1=ALU.add,
                 )
-                scaled_t[state, chunk] = scaled[:, j, :]
+                scaled_cm[state, chunk] = scaled[:, j, :]
 
         def turn_for_stats(state, t):
             for half in range(HALVES):
-                turned = bank(STAT_BANKS[len(stat_banks) % len(STAT_BANKS)], [P, BANK], F32)
+                turned = bank(STAT_BANKS[len(stat_tiles) % len(STAT_BANKS)], [P, BANK], F32)
                 for c in range(CHUNKS_PER_HALF):
                     nc.tensor.transpose(
                         turned[:, c * P : (c + 1) * P],
-                        sup_t[state, half * CHUNKS_PER_HALF + c][:, t * P : (t + 1) * P],
+                        sup_cm[state, half * CHUNKS_PER_HALF + c][:, t * P : (t + 1) * P],
                         ident_f32[:],
                     )
-                stat_banks[state, t, half] = turned
+                stat_tiles[state, t, half] = turned
 
         def row_partials(state, t):
             if t == 0:
-                mean_var = stream.tile([P, ROW_TILES, 2], F32, bufs=2)
-                pairs = stream.tile([P, ROW_TILES, 2], F32, bufs=2)
+                mean_var = stream.tile([P, ROW_TILES, 2], F32)
+                pairs = stream.tile([P, ROW_TILES, 2], F32)
                 rstd = stream.tile([P, ROW_TILES], F32, bufs=3)
                 moments[state] = mean_var
-                spread[state] = pairs
+                neg_mean_std[state] = pairs
                 inv_std[state] = rstd
-            partial = stream.tile([P, HALVES, 6], F32, bufs=2)
+            partial = stream.tile([P, HALVES, 6], F32)
             for half in range(HALVES):
-                nc.vector.bn_stats(out=partial[:, half, :], in_=stat_banks[state, t, half][:])
+                nc.vector.bn_stats(out=partial[:, half, :], in_=stat_tiles[state, t, half][:])
             partials[state, t] = partial
 
         def row_moments(state, t):
@@ -320,57 +325,58 @@ def tile_quantumsuperposition_kernel(
 
         def row_std(state, first, last):
             nc.scalar.activation(
-                out=spread[state][:, first:last, 1], in_=moments[state][:, first:last, 1], func=ACT.Sqrt, bias=eps[:]
+                out=neg_mean_std[state][:, first:last, 1],
+                in_=moments[state][:, first:last, 1],
+                func=ACT.Sqrt,
+                bias=eps[:],
             )
 
-        def row_rstd(state, first, last):
-            nc.vector.reciprocal(out=inv_std[state][:, first:last], in_=spread[state][:, first:last, 1])
+        def row_inv_std(state, first, last):
+            nc.vector.reciprocal(out=inv_std[state][:, first:last], in_=neg_mean_std[state][:, first:last, 1])
 
         def negate_means(state):
-            count = folded(state)
             nc.scalar.activation(
-                out=spread[state][:, 0:count, 0], in_=moments[state][:, 0:count, 0], func=ACT.Copy, scale=-1.0
+                out=neg_mean_std[state][:, 0:FOLDED, 0], in_=moments[state][:, 0:FOLDED, 0], func=ACT.Copy, scale=-1.0
             )
 
-        def split_moments(state):
-            count = folded(state)
-            terms = split_cols[:, 0 : 2 * count * SPLIT].rearrange("p (v j) -> p v j", j=SPLIT)
-            left = spread[state][:, 0:count, :].rearrange("p t w -> p (t w)")
-            for j in range(SPLIT):
-                nc.gpsimd.tensor_copy(out=terms[:, :, j], in_=left)
-                if j + 1 < SPLIT:
-                    remainder = stream.tile([P, 2 * count], F32, bufs=2)
-                    nc.gpsimd.tensor_tensor(out=remainder[:], in0=left, in1=terms[:, :, j], op=ALU.subtract)
-                    left = remainder[:]
+        def split_terms(state):
+            terms = term_cols[:, 0 : 2 * FOLDED * TERMS].rearrange("p (v j) -> p v j", j=TERMS)
+            values = neg_mean_std[state][:, 0:FOLDED, :].rearrange("p t w -> p (t w)")
+            remainder = stream.tile([P, 2 * FOLDED], F32)
+            nc.gpsimd.tensor_copy(out=terms[:, :, 0], in_=values)
+            nc.gpsimd.tensor_tensor(out=remainder[:], in0=values, in1=terms[:, :, 0], op=ALU.subtract)
+            nc.gpsimd.tensor_copy(out=terms[:, :, 1], in_=remainder[:])
+            nc.gpsimd.tensor_tensor(out=terms[:, :, 2], in0=remainder[:], in1=terms[:, :, 1], op=ALU.subtract)
 
         def next_fold_bank(shape, dtype):
-            fold_turns.append(len(fold_turns))
-            ring = FOLD_BANKS + (0, 1) if TAILB and len(products) == S * CHUNKS else FOLD_BANKS
-            return bank(ring[fold_turns[-1] % len(ring)], shape, dtype)
+            multiplies_done = len(products) == S * CHUNKS
+            banks = FOLD_BANKS + PRODUCT_BANKS if multiplies_done else FOLD_BANKS
+            fold_turns.append(banks[len(fold_turns) % len(banks)])
+            return bank(fold_turns[-1], shape, dtype)
 
-        def turn_split(state):
-            turned = next_fold_bank([P, P], BF16)
-            nc.tensor.transpose(turned[:], split_cols[:], ident_bf16[:])
-            lhs = stream.tile([P, P], BF16, bufs=2)
-            nc.scalar.copy(out=lhs[:], in_=turned[:])
+        def turn_terms(state):
+            terms_turned = next_fold_bank([P, P], BF16)
+            nc.tensor.transpose(terms_turned[:], term_cols[:], ident_bf16[:])
+            lhs = stream.tile([P, P], BF16)
+            nc.scalar.copy(out=lhs[:], in_=terms_turned[:])
             fold_lhs[state] = lhs
 
         def turn_and_fold(state, t):
             for half in range(HALVES):
-                turned = next_fold_bank([P, BANK], F32)
+                folded = next_fold_bank([P, BANK], F32)
                 for c in range(CHUNKS_PER_HALF):
                     nc.tensor.matmul(
-                        out=turned[:, c * P : (c + 1) * P],
-                        lhsT=scaled_t[state, half * CHUNKS_PER_HALF + c][:, t * P : (t + 1) * P],
+                        out=folded[:, c * P : (c + 1) * P],
+                        lhsT=scaled_cm[state, half * CHUNKS_PER_HALF + c][:, t * P : (t + 1) * P],
                         rhs=ident_f32[:],
                         start=(c == 0),
                         stop=False,
                         is_transpose=True,
                     )
-                fold_banks[state, t, half] = turned
+                fold_tiles[state, t, half] = folded
             for half in range(HALVES):
                 nc.tensor.matmul(
-                    out=fold_banks[state, t, half][:],
+                    out=fold_tiles[state, t, half][:],
                     lhsT=fold_lhs[state][:],
                     rhs=fold_rhs[:, t, half * BANK : (half + 1) * BANK],
                     start=False,
@@ -383,121 +389,116 @@ def tile_quantumsuperposition_kernel(
         def finish_folded(state, t):
             result = stream.tile([P, Q], F32, bufs=RESULT_BUFS)
             results[state, t] = result
-            rstd = inv_std[state][:, t : t + 1]
+            rstd_col = inv_std[state][:, t : t + 1]
             for half in range(HALVES):
                 dst = result[:, half * BANK : (half + 1) * BANK]
-                src = fold_banks[state, t, half][:]
+                src = fold_tiles[state, t, half][:]
                 if state == S - 1 and half == 1:
-                    nc.vector.tensor_scalar(out=dst, in0=src, scalar1=rstd, scalar2=None, op0=ALU.mult)
+                    nc.vector.tensor_scalar(out=dst, in0=src, scalar1=rstd_col, scalar2=None, op0=ALU.mult)
                 else:
-                    nc.scalar.activation(out=dst, in_=src, func=ACT.Copy, scale=rstd)
+                    nc.scalar.activation(out=dst, in_=src, func=ACT.Copy, scale=rstd_col)
             store(state, t)
 
-        def centre_plain(state, t):
+        def centre_plain(state):
             result = stream.tile([P, Q], F32, bufs=RESULT_BUFS)
-            results[state, t] = result
+            results[state, PLAIN] = result
             for half in range(HALVES):
                 span = slice(half * BANK, (half + 1) * BANK)
                 nc.vector.scalar_tensor_tensor(
                     out=result[:, span],
-                    in0=stat_banks[state, t, half][:],
-                    scalar=moments[state][:, t, 0:1],
+                    in0=stat_tiles[state, PLAIN, half][:],
+                    scalar=moments[state][:, PLAIN, 0:1],
                     in1=gamma_all[:, span],
                     op0=ALU.subtract,
                     op1=ALU.mult,
                 )
 
-        def finish_plain(state, t):
+        def finish_plain(state):
             nc.vector.scalar_tensor_tensor(
-                out=results[state, t][:],
-                in0=results[state, t][:],
-                scalar=inv_std[state][:, t : t + 1],
+                out=results[state, PLAIN][:],
+                in0=results[state, PLAIN][:],
+                scalar=inv_std[state][:, PLAIN : PLAIN + 1],
                 in1=beta_all[:],
                 op0=ALU.mult,
                 op1=ALU.add,
             )
-            store(state, t)
+            store(state, PLAIN)
 
-        tiles = [(state, t) for state in range(S) for t in range(ROW_TILES)]
-        turn_step = {(state, t): STEPS * (state + 1) + t for state, t in tiles}
-        split_step = {state: turn_step[state, folded(state) - 1] + 1 for state in range(S) if folded(state)}
-        fold_step = {(state, t): split_step[state] + SPLIT_LAG + 1 + t for state, t in tiles if t < folded(state)}
-        last_step = max(max(fold_step.values()) + 1, max(turn_step.values()) + 2)
+        turn_step = {(state, t): STEPS * (state + 1) + t for state in range(S) for t in range(ROW_TILES)}
+        centre_step = {state: turn_step[state, PLAIN] + 1 for state in range(S)}
+        std_step = {state: turn_step[state, FOLDED - 1] + 1 for state in range(S)}
+        fold_step = {(state, t): std_step[state] + SPLIT_LAG + 1 + t for state in range(S) for t in range(FOLDED)}
+        last_step = max(fold_step.values()) + 1
 
         def due(table, step):
             return [key for key in table if table[key] == step]
 
+        def vector_share(step):
+            piece = step + COPY_AHEAD
+            if piece < PASSES:
+                return BANK
+            if piece == PASSES:
+                return 0
+            if not due(turn_step, step - 1):
+                return SHARE_NO_STATS
+            share = SHARE_FINISH if due(fold_step, step - 1) else SHARE_NO_FINISH
+            return share - SHARE_PLAIN_COST * len(due(centre_step, step) + due(centre_step, step - 1))
+
         for step in range(-LOAD_AHEAD, last_step + 1):
-            slot, i = divmod(step, STEPS)
+            state_now, pair_now = divmod(step, STEPS)
+            copy_piece = step + COPY_AHEAD
+            quant_piece = step + QUANT_AHEAD
+            copying = 0 <= copy_piece < PIECES
+            measured = due(turn_step, step - 1)
+
             if step + LOAD_AHEAD < PIECES:
                 load_piece(step + LOAD_AHEAD)
             if step == 0:
-                load_late_constants()
-            copy_piece = step + COPY_AHEAD
-            copying = 0 <= copy_piece < PIECES
-            measured = due(turn_step, step - 1)
-            plain = [(state, t) for state, t in measured if t >= folded(state)]
-
-            closing = [(state, t) for state, t in due(turn_step, step - 2) if t >= folded(state)]
-            if copy_piece < 2:
-                cut = BANK
-            elif copy_piece == 2:
-                cut = 0
-            elif not measured:
-                cut = CUT0
-            else:
-                cut = (CUT2 if due(fold_step, step - 1) else CUT1) - CUT3 * (len(plain) + len(closing))
-            if step + QUANT_AHEAD == 0:
-                mix_weights()
-            if 0 <= step + QUANT_AHEAD < PIECES:
-                quantize_piece(step + QUANT_AHEAD)
-            if step + QUANT_AHEAD == 0:
+                load_norm_vectors()
+            if quant_piece == 0:
+                make_mix()
+            if 0 <= quant_piece < PIECES:
+                quantize_piece(quant_piece)
+            if quant_piece == 0:
                 quantize_features(0)
-                mix_bias()
+                make_bias_mix()
                 quantize_features(1)
-            gslot, gi = divmod(step - GAMMA_LAG, STEPS)
-            if 0 <= gslot < S and folded(gslot):
-                apply_gamma(gslot, gi, step + QUANT_AHEAD)
-            for state in due(split_step, step - 1):
-                if LATE:
-                    split_moments(state)
+            gamma_state, gamma_pair = divmod(step - GAMMA_LAG, STEPS)
+            if 0 <= gamma_state < S:
+                apply_gamma(gamma_state, gamma_pair, quant_piece)
+            for state in due(std_step, step - 1):
+                split_terms(state)
             for state, t in measured:
                 row_partials(state, t)
             for state, t in due(fold_step, step - 1):
                 finish_folded(state, t)
-            if 0 <= slot < S:
-                for chunk in (2 * i, 2 * i + 1):
-                    multiply(slot, chunk)
-                for chunk in (2 * i, 2 * i + 1):
-                    apply_mix(slot, chunk)
-            for state, t in due(turn_step, step - 2):
-                if t >= folded(state):
-                    row_rstd(state, t, t + 1)
-            for state in due(split_step, step - 1):
-                row_rstd(state, 0, folded(state))
-            if copying and not ORD:
-                interleave(copy_piece, nc.vector.tensor_copy, 0, cut)
+            if 0 <= state_now < S:
+                for chunk in (2 * pair_now, 2 * pair_now + 1):
+                    multiply(state_now, chunk)
+                for chunk in (2 * pair_now, 2 * pair_now + 1):
+                    apply_mix(state_now, chunk)
+            for state in due(centre_step, step - 1):
+                row_inv_std(state, PLAIN, PLAIN + 1)
+            for state in due(std_step, step - 1):
+                row_inv_std(state, 0, FOLDED)
             for state, t in measured:
                 row_moments(state, t)
-            if copying and ORD:
-                interleave(copy_piece, nc.vector.tensor_copy, 0, cut)
-            for state, t in due(turn_step, step - 2):
-                if t >= folded(state):
-                    finish_plain(state, t)
-            for state, t in plain:
-                centre_plain(state, t)
             if copying:
-                interleave(copy_piece, nc.scalar.copy, cut, BANK)
-            for state in due(split_step, step):
-                row_std(state, 0, folded(state))
+                interleave(copy_piece, nc.vector.tensor_copy, 0, vector_share(step))
+            for state in due(centre_step, step - 1):
+                finish_plain(state)
+            for state in due(centre_step, step):
+                centre_plain(state)
+            if copying:
+                interleave(copy_piece, nc.scalar.copy, vector_share(step), BANK)
+            for state in due(std_step, step):
+                row_std(state, 0, FOLDED)
                 negate_means(state)
-                if not LATE:
-                    split_moments(state)
-            for state, t in plain:
-                row_std(state, t, t + 1)
+            for state in due(centre_step, step):
+                row_std(state, PLAIN, PLAIN + 1)
             for state, t in due(turn_step, step):
                 turn_for_stats(state, t)
-            for state in due(split_step, step - SPLIT_LAG):
-                turn_split(state)
+            for state in due(std_step, step - SPLIT_LAG):
+                turn_terms(state)
             for state, t in due(fold_step, step):
                 turn_and_fold(state, t)

import math
from contextlib import ExitStack

import concourse.mybir as mybir
from concourse.masks import make_identity

B, S, I, Q = 512, 8, 1024, 1024
LN_EPS = 1e-5
FLOPS = 2 * B * S * I * Q

F32 = mybir.dt.float32
BF16 = mybir.dt.bfloat16
I32 = mybir.dt.int32
U32 = mybir.dt.uint32
U8 = mybir.dt.uint8
FP8X4 = mybir.dt.float8_e5m2_x4
ALU = mybir.AluOpType
ACT = mybir.ActivationFunctionType
AXIS = mybir.AxisListType

P = 128
PACK = 4
K_PASS = P * PACK
PASSES = I // K_PASS
BANK = 512
HALVES = Q // BANK
CHUNKS = Q // P
CHUNKS_PER_HALF = BANK // P
ROW_TILES = B // P
FOLDED = ROW_TILES - 1
PLAIN = ROW_TILES - 1
TERMS = 3
GROUP = 4

STEPS = ROW_TILES
PIECES = S * PASSES * HALVES
LOAD_AHEAD = 8
COPY_AHEAD = 4
QUANT_AHEAD = 2
GAMMA_LAG = 5
SPLIT_LAG = 2

RING = 11
RAW_BUFS = 7
CODE_BUFS = 7
RESULT_BUFS = 5

PRODUCT_BANKS = (0, 1)
STAT_BANKS = (2, 3, 4, 5)
FOLD_BANKS = (6, 7)

SHARE_NO_STATS = 416
SHARE_NO_FINISH = 224
SHARE_FINISH = 352
SHARE_PLAIN_COST = 112

TWO_PI_HI = 6.28125
TWO_PI_LO = 2.0 * math.pi - TWO_PI_HI
SIN_FLOOR = -3.1415925


def tile_quantumsuperposition_kernel(
    tc, language_features, W, b, amplitude_weights, phase_weights, ln_gamma, ln_beta, out
):
    nc = tc.nc

    with ExitStack() as ctx:
        keep = ctx.enter_context(tc.tile_pool(name="keep", bufs=1))
        stream = ctx.enter_context(tc.tile_pool(name="stream", bufs=2))
        psum = ctx.enter_context(tc.psum_pool(name="psum", bufs=1))
        ctx.enter_context(tc.manual_schedule())

        def bank(index, shape, dtype):
            return psum.tile(shape, dtype, name="bank%d" % index, tag="bank%d" % index)

        ident_f32 = keep.tile([P, P], F32)
        ident_bf16 = keep.tile([P, P], BF16)
        make_identity(nc, ident_bf16[:])
        make_identity(nc, ident_f32[:])

        per_state = S * CHUNKS
        rows_amp_phase = keep.tile([P, P], BF16)
        rows_bias_gamma = keep.tile([P, P], BF16)
        nc.vector.memset(rows_bias_gamma[:], 0.0)
        as_rows = "s (c p) -> (s c) p"
        nc.scalar.dma_start(out=rows_amp_phase[0:per_state, :], in_=amplitude_weights.rearrange(as_rows, p=P))
        nc.scalar.dma_start(out=rows_amp_phase[per_state:P, :], in_=phase_weights.rearrange(as_rows, p=P))
        nc.scalar.dma_start(out=rows_bias_gamma[0:per_state, :], in_=b.rearrange(as_rows, p=P))
        nc.scalar.dma_start(
            out=rows_bias_gamma[per_state : per_state + CHUNKS, :], in_=ln_gamma.rearrange("(c p) -> c p", p=P)
        )

        x_rows = keep.tile([P, ROW_TILES, I], BF16)
        x_hbm = language_features.rearrange("(t p) k -> p t k", p=P)
        for pair in range(ROW_TILES // 2):
            nc.sync.dma_start(out=x_rows[:, 2 * pair : 2 * pair + 2, :], in_=x_hbm[:, 2 * pair : 2 * pair + 2, :])

        one = keep.tile([P, 1], F32)
        eps = keep.tile([P, 1], F32)
        nc.vector.memset(one[:], 1.0)
        nc.vector.tensor_scalar(out=eps[:], in0=one[:], scalar1=LN_EPS, scalar2=None, op0=ALU.mult)

        term_cols = keep.tile([P, P], BF16)
        nc.gpsimd.memset(term_cols[:], 0.0)
        fold_rhs = keep.tile([P, FOLDED, Q], BF16)
        nc.vector.memset(fold_rhs[:], 0.0)

        small_turned = bank(FOLD_BANKS[0], [P, 2 * P], BF16)
        nc.tensor.transpose(small_turned[:, 0:P], rows_amp_phase[:], ident_bf16[:])
        nc.tensor.transpose(small_turned[:, P : 2 * P], rows_bias_gamma[:], ident_bf16[:])
        small = keep.tile([P, 2 * P], F32)
        nc.vector.tensor_copy(out=small[:], in_=small_turned[:])
        amp_cm = small[:, 0:per_state]
        phase_cm = small[:, per_state:P]
        bias_cm = small[:, P : P + per_state]
        gamma_cm = small[:, P + per_state : P + per_state + CHUNKS]

        top = keep.tile([P, 1, CHUNKS], F32)
        shifted = keep.tile([P, S, CHUNKS], F32)
        expd = keep.tile([P, S, CHUNKS], F32)
        total = keep.tile([P, CHUNKS], F32)
        inv_total = keep.tile([P, 1, CHUNKS], F32)
        amplitudes = keep.tile([P, S, CHUNKS], F32)
        phase_abs = keep.tile([P, per_state], F32)
        turns_f32 = keep.tile([P, per_state], F32)
        turns = keep.tile([P, per_state], I32)
        rest_hi = keep.tile([P, per_state], F32)
        rest = keep.tile([P, per_state], F32)
        rest_neg_abs = keep.tile([P, per_state], F32)
        angle = keep.tile([P, per_state], F32)
        cosine = keep.tile([P, per_state], F32)
        mix = keep.tile([P, per_state], F32)
        bias_mix = keep.tile([P, per_state], F32)
        nc.vector.tensor_reduce(
            out=top[:, 0, :], in_=amp_cm.rearrange("p (s c) -> p c s", c=CHUNKS), axis=AXIS.X, op=ALU.max
        )
        nc.vector.scalar_tensor_tensor(
            out=phase_abs[:], in0=phase_cm, scalar=-1.0, in1=phase_cm, op0=ALU.mult, op1=ALU.max
        )
        nc.vector.tensor_tensor(
            out=shifted[:],
            in0=amp_cm.rearrange("p (s c) -> p s c", c=CHUNKS),
            in1=top[:].to_broadcast([P, S, CHUNKS]),
            op=ALU.subtract,
        )
        nc.vector.tensor_scalar(
            out=turns_f32[:], in0=phase_abs[:], scalar1=1.0 / (2.0 * math.pi), scalar2=0.25, op0=ALU.mult, op1=ALU.add
        )
        nc.scalar.activation(out=expd[:], in_=shifted[:], func=ACT.Exp)
        nc.vector.tensor_copy(out=turns[:], in_=turns_f32[:])
        nc.vector.tensor_reduce(out=total[:], in_=expd[:].rearrange("p s c -> p c s"), axis=AXIS.X, op=ALU.add)
        nc.vector.scalar_tensor_tensor(
            out=rest_hi[:], in0=turns[:], scalar=-TWO_PI_HI, in1=phase_abs[:], op0=ALU.mult, op1=ALU.add
        )
        nc.vector.reciprocal(out=inv_total[:, 0, :], in_=total[:])
        nc.vector.scalar_tensor_tensor(
            out=rest[:], in0=turns[:], scalar=-TWO_PI_LO, in1=rest_hi[:], op0=ALU.mult, op1=ALU.add
        )
        nc.vector.tensor_tensor(
            out=amplitudes[:], in0=expd[:], in1=inv_total[:].to_broadcast([P, S, CHUNKS]), op=ALU.mult
        )
        nc.vector.scalar_tensor_tensor(
            out=rest_neg_abs[:], in0=rest[:], scalar=-1.0, in1=rest[:], op0=ALU.mult, op1=ALU.min
        )
        nc.vector.tensor_scalar(
            out=angle[:], in0=rest_neg_abs[:], scalar1=math.pi / 2.0, scalar2=SIN_FLOOR, op0=ALU.add, op1=ALU.max
        )
        nc.scalar.activation(out=cosine[:], in_=angle[:], func=ACT.Sin)

        def make_mix():
            nc.vector.tensor_tensor(
                out=mix[:], in0=amplitudes[:].rearrange("p s c -> p (s c)"), in1=cosine[:], op=ALU.mult
            )

        def make_bias_mix():
            nc.vector.tensor_tensor(out=bias_mix[:], in0=bias_cm, in1=mix[:], op=ALU.mult)

        x_grouped = keep.tile([P, PASSES, B, PACK], BF16, align_bytes=64)
        x_codes = keep.tile([P, PASSES, B], U32, align_bytes=64)
        x_scales = keep.tile([P, PASSES, B], U8, align_bytes=64)
        words_per_pass = K_PASS // 2
        for pair in range(ROW_TILES // 2):
            for g in range(PASSES):
                x_turned = bank(STAT_BANKS[PASSES * pair + g], [P, 2, 2, P], F32)
                for t in range(2):
                    words = x_rows[:, 2 * pair + t, :].bitcast(F32)
                    for u in range(2):
                        nc.tensor.transpose(
                            x_turned[:, t, u, :],
                            words[:, words_per_pass * g + u : words_per_pass * (g + 1) : 2],
                            ident_f32[:],
                        )
                dst = x_grouped[:, g, 2 * P * pair : 2 * P * (pair + 1), :].rearrange("p r j -> p (r j)").bitcast(F32)
                nc.scalar.copy(
                    out=dst.rearrange("p (t r u) -> p t r u", t=2, u=2),
                    in_=x_turned[:].rearrange("p t u r -> p t r u"),
                )

        def quantize_features(g):
            nc.vector.quantize_mx(
                out=x_codes[:, g, :].bitcast(FP8X4),
                scales=x_scales[:, g, :],
                in_=x_grouped[:, g, :, :].rearrange("p r j -> p (r j)"),
            )

        gamma_all = keep.tile([P, Q], BF16)
        beta_all = keep.tile([P, Q], BF16)

        def load_norm_vectors():
            nc.sync.dma_start(out=gamma_all[:], in_=ln_gamma.partition_broadcast(P))
            nc.sync.dma_start(out=beta_all[:], in_=ln_beta.partition_broadcast(P))
            for t in range(FOLDED):
                row = 2 * TERMS * t
                nc.sync.dma_start(out=fold_rhs[row : row + TERMS, t, :], in_=ln_gamma.partition_broadcast(TERMS))
                nc.sync.dma_start(
                    out=fold_rhs[row + TERMS : row + 2 * TERMS, t, :], in_=ln_beta.partition_broadcast(TERMS)
                )

        w_raw, w_grouped, w_codes, w_scales = {}, {}, {}, {}
        products, sup_cm, scaled_cm = {}, {}, {}
        stat_tiles, partials, moments, neg_mean_std, inv_std = {}, {}, {}, {}, {}
        fold_lhs, fold_tiles, results = {}, {}, {}
        fold_turns = []

        def piece_place(piece):
            state, j = divmod(piece, PASSES * HALVES)
            return state, j % PASSES, j // PASSES

        def ring_tile(piece, shape, dtype):
            name = "ring%d" % (piece % RING)
            return keep.tile(shape, dtype, name=name, tag=name, align_bytes=64)

        def load_piece(piece):
            state, g, half = piece_place(piece)
            raw = stream.tile([P, PACK, BANK], BF16, bufs=RAW_BUFS)
            rows = W[state, g * K_PASS : (g + 1) * K_PASS, half * BANK : (half + 1) * BANK]
            nc.sync.dma_start(out=raw[:], in_=rows.rearrange("(p j) n -> p j n", j=PACK))
            w_raw[piece] = raw

        def interleave(piece, copy, first, last):
            if piece not in w_grouped:
                w_grouped[piece] = ring_tile(piece, [P, BANK, PACK], BF16)
            if last > first:
                copy(
                    out=w_grouped[piece][:, first:last, :].rearrange("p (c i) j -> p c j i", i=GROUP),
                    in_=w_raw[piece][:, :, first:last].rearrange("p j (c i) -> p c j i", i=GROUP),
                )

        def quantize_piece(piece):
            codes = stream.tile([P, BANK], U32, bufs=CODE_BUFS, align_bytes=64)
            scales = stream.tile([P, BANK], U8, bufs=CODE_BUFS, align_bytes=64)
            nc.vector.quantize_mx(
                out=codes[:].bitcast(FP8X4), scales=scales[:], in_=w_grouped[piece][:].rearrange("p n j -> p (n j)")
            )
            w_codes[piece_place(piece)] = codes
            w_scales[piece_place(piece)] = scales

        def multiply(state, chunk):
            half, c = divmod(chunk, CHUNKS_PER_HALF)
            acc = bank(PRODUCT_BANKS[chunk % len(PRODUCT_BANKS)], [P, B], F32)
            for g in range(PASSES):
                nc.tensor.matmul_mx(
                    out=acc[:],
                    lhsT=w_codes[state, g, half][:, c * P : (c + 1) * P].bitcast(FP8X4),
                    lhsT_scale=w_scales[state, g, half][:, c * P : (c + 1) * P],
                    rhs=x_codes[:, g, :].bitcast(FP8X4),
                    rhs_scale=x_scales[:, g, :],
                    start=(g == 0),
                    stop=(g == PASSES - 1),
                )
            products[state, chunk] = acc

        def apply_mix(state, chunk):
            sup = stream.tile([P, B], F32, bufs=2 * CHUNKS)
            col = state * CHUNKS + chunk
            nc.scalar.activation(
                out=sup[:],
                in_=products[state, chunk][:],
                func=ACT.Identity,
                scale=mix[:, col : col + 1],
                bias=bias_mix[:, col : col + 1],
            )
            sup_cm[state, chunk] = sup

        def apply_gamma(state, pair, piece):
            scaled = ring_tile(piece, [P, 2, B], F32)
            for j in range(2):
                chunk = 2 * pair + j
                nc.gpsimd.tensor_scalar(
                    out=scaled[:, j, 0 : FOLDED * P],
                    in0=sup_cm[state, chunk][:, 0 : FOLDED * P],
                    scalar1=gamma_cm[:, chunk : chunk + 1],
                    scalar2=0.0,
                    op0=ALU.mult,
                    op1=ALU.add,
                )
                scaled_cm[state, chunk] = scaled[:, j, :]

        def turn_for_stats(state, t):
            for half in range(HALVES):
                turned = bank(STAT_BANKS[len(stat_tiles) % len(STAT_BANKS)], [P, BANK], F32)
                for c in range(CHUNKS_PER_HALF):
                    nc.tensor.transpose(
                        turned[:, c * P : (c + 1) * P],
                        sup_cm[state, half * CHUNKS_PER_HALF + c][:, t * P : (t + 1) * P],
                        ident_f32[:],
                    )
                stat_tiles[state, t, half] = turned

        def row_partials(state, t):
            if t == 0:
                mean_var = stream.tile([P, ROW_TILES, 2], F32)
                pairs = stream.tile([P, ROW_TILES, 2], F32)
                rstd = stream.tile([P, ROW_TILES], F32, bufs=3)
                moments[state] = mean_var
                neg_mean_std[state] = pairs
                inv_std[state] = rstd
            partial = stream.tile([P, HALVES, 6], F32)
            for half in range(HALVES):
                nc.vector.bn_stats(out=partial[:, half, :], in_=stat_tiles[state, t, half][:])
            partials[state, t] = partial

        def row_moments(state, t):
            nc.vector.bn_aggr(out=moments[state][:, t, :], in_=partials[state, t][:].rearrange("p h j -> p (h j)"))

        def row_std(state, first, last):
            nc.scalar.activation(
                out=neg_mean_std[state][:, first:last, 1],
                in_=moments[state][:, first:last, 1],
                func=ACT.Sqrt,
                bias=eps[:],
            )

        def row_inv_std(state, first, last):
            nc.vector.reciprocal(out=inv_std[state][:, first:last], in_=neg_mean_std[state][:, first:last, 1])

        def negate_means(state):
            nc.scalar.activation(
                out=neg_mean_std[state][:, 0:FOLDED, 0], in_=moments[state][:, 0:FOLDED, 0], func=ACT.Copy, scale=-1.0
            )

        def split_terms(state):
            terms = term_cols[:, 0 : 2 * FOLDED * TERMS].rearrange("p (v j) -> p v j", j=TERMS)
            values = neg_mean_std[state][:, 0:FOLDED, :].rearrange("p t w -> p (t w)")
            remainder = stream.tile([P, 2 * FOLDED], F32)
            nc.gpsimd.tensor_copy(out=terms[:, :, 0], in_=values)
            nc.gpsimd.tensor_tensor(out=remainder[:], in0=values, in1=terms[:, :, 0], op=ALU.subtract)
            nc.gpsimd.tensor_copy(out=terms[:, :, 1], in_=remainder[:])
            nc.gpsimd.tensor_tensor(out=terms[:, :, 2], in0=remainder[:], in1=terms[:, :, 1], op=ALU.subtract)

        def next_fold_bank(shape, dtype):
            multiplies_done = len(products) == S * CHUNKS
            banks = FOLD_BANKS + PRODUCT_BANKS if multiplies_done else FOLD_BANKS
            fold_turns.append(banks[len(fold_turns) % len(banks)])
            return bank(fold_turns[-1], shape, dtype)

        def turn_terms(state):
            terms_turned = next_fold_bank([P, P], BF16)
            nc.tensor.transpose(terms_turned[:], term_cols[:], ident_bf16[:])
            lhs = stream.tile([P, P], BF16)
            nc.scalar.copy(out=lhs[:], in_=terms_turned[:])
            fold_lhs[state] = lhs

        def turn_and_fold(state, t):
            for half in range(HALVES):
                folded = next_fold_bank([P, BANK], F32)
                for c in range(CHUNKS_PER_HALF):
                    nc.tensor.matmul(
                        out=folded[:, c * P : (c + 1) * P],
                        lhsT=scaled_cm[state, half * CHUNKS_PER_HALF + c][:, t * P : (t + 1) * P],
                        rhs=ident_f32[:],
                        start=(c == 0),
                        stop=False,
                        is_transpose=True,
                    )
                fold_tiles[state, t, half] = folded
            for half in range(HALVES):
                nc.tensor.matmul(
                    out=fold_tiles[state, t, half][:],
                    lhsT=fold_lhs[state][:],
                    rhs=fold_rhs[:, t, half * BANK : (half + 1) * BANK],
                    start=False,
                    stop=True,
                )

        def store(state, t):
            nc.sync.dma_start(out=out[t * P : (t + 1) * P, state, :], in_=results[state, t][:])

        def finish_folded(state, t):
            result = stream.tile([P, Q], F32, bufs=RESULT_BUFS)
            results[state, t] = result
            rstd_col = inv_std[state][:, t : t + 1]
            for half in range(HALVES):
                dst = result[:, half * BANK : (half + 1) * BANK]
                src = fold_tiles[state, t, half][:]
                if state == S - 1 and half == 1:
                    nc.vector.tensor_scalar(out=dst, in0=src, scalar1=rstd_col, scalar2=None, op0=ALU.mult)
                else:
                    nc.scalar.activation(out=dst, in_=src, func=ACT.Copy, scale=rstd_col)
            store(state, t)

        def centre_plain(state):
            result = stream.tile([P, Q], F32, bufs=RESULT_BUFS)
            results[state, PLAIN] = result
            for half in range(HALVES):
                span = slice(half * BANK, (half + 1) * BANK)
                nc.vector.scalar_tensor_tensor(
                    out=result[:, span],
                    in0=stat_tiles[state, PLAIN, half][:],
                    scalar=moments[state][:, PLAIN, 0:1],
                    in1=gamma_all[:, span],
                    op0=ALU.subtract,
                    op1=ALU.mult,
                )

        def finish_plain(state):
            nc.vector.scalar_tensor_tensor(
                out=results[state, PLAIN][:],
                in0=results[state, PLAIN][:],
                scalar=inv_std[state][:, PLAIN : PLAIN + 1],
                in1=beta_all[:],
                op0=ALU.mult,
                op1=ALU.add,
            )
            store(state, PLAIN)

        turn_step = {(state, t): STEPS * (state + 1) + t for state in range(S) for t in range(ROW_TILES)}
        centre_step = {state: turn_step[state, PLAIN] + 1 for state in range(S)}
        std_step = {state: turn_step[state, FOLDED - 1] + 1 for state in range(S)}
        fold_step = {(state, t): std_step[state] + SPLIT_LAG + 1 + t for state in range(S) for t in range(FOLDED)}
        last_step = max(fold_step.values()) + 1

        def due(table, step):
            return [key for key in table if table[key] == step]

        def vector_share(step):
            piece = step + COPY_AHEAD
            if piece < PASSES:
                return BANK
            if piece == PASSES:
                return 0
            if not due(turn_step, step - 1):
                return SHARE_NO_STATS
            share = SHARE_FINISH if due(fold_step, step - 1) else SHARE_NO_FINISH
            return share - SHARE_PLAIN_COST * len(due(centre_step, step) + due(centre_step, step - 1))

        for step in range(-LOAD_AHEAD, last_step + 1):
            state_now, pair_now = divmod(step, STEPS)
            copy_piece = step + COPY_AHEAD
            quant_piece = step + QUANT_AHEAD
            copying = 0 <= copy_piece < PIECES
            measured = due(turn_step, step - 1)

            if step + LOAD_AHEAD < PIECES:
                load_piece(step + LOAD_AHEAD)
            if step == 0:
                load_norm_vectors()
            if quant_piece == 0:
                make_mix()
            if 0 <= quant_piece < PIECES:
                quantize_piece(quant_piece)
            if quant_piece == 0:
                quantize_features(0)
                make_bias_mix()
                quantize_features(1)
            gamma_state, gamma_pair = divmod(step - GAMMA_LAG, STEPS)
            if 0 <= gamma_state < S:
                apply_gamma(gamma_state, gamma_pair, quant_piece)
            for state in due(std_step, step - 1):
                split_terms(state)
            for state, t in measured:
                row_partials(state, t)
            for state, t in due(fold_step, step - 1):
                finish_folded(state, t)
            if 0 <= state_now < S:
                for chunk in (2 * pair_now, 2 * pair_now + 1):
                    multiply(state_now, chunk)
                for chunk in (2 * pair_now, 2 * pair_now + 1):
                    apply_mix(state_now, chunk)
            for state in due(centre_step, step - 1):
                row_inv_std(state, PLAIN, PLAIN + 1)
            for state in due(std_step, step - 1):
                row_inv_std(state, 0, FOLDED)
            for state, t in measured:
                row_moments(state, t)
            if copying:
                interleave(copy_piece, nc.vector.tensor_copy, 0, vector_share(step))
            for state in due(centre_step, step - 1):
                finish_plain(state)
            for state in due(centre_step, step):
                centre_plain(state)
            if copying:
                interleave(copy_piece, nc.scalar.copy, vector_share(step), BANK)
            for state in due(std_step, step):
                row_std(state, 0, FOLDED)
                negate_means(state)
            for state in due(centre_step, step):
                row_std(state, PLAIN, PLAIN + 1)
            for state, t in due(turn_step, step):
                turn_for_stats(state, t)
            for state in due(std_step, step - SPLIT_LAG):
                turn_terms(state)
            for state, t in due(fold_step, step):
                turn_and_fold(state, t)
